import numpy as np
import ml_dtypes


def mxq(x, axis, fmt="e4m3"):
    dtype, down = {"e4m3": (ml_dtypes.float8_e4m3fn, 7), "e5m2": (ml_dtypes.float8_e5m2, 14)}[fmt]
    v = np.moveaxis(np.asarray(x, np.float32).astype(ml_dtypes.bfloat16).astype(np.float64), axis, -1)
    blocks = v.reshape(v.shape[:-1] + (-1, 32))
    amax = np.abs(blocks).max(-1, keepdims=True)
    byte = np.maximum(np.where(amax > 0, np.frexp(amax)[1] - 1 + 127, 0) - down, 1)
    scale = np.exp2(byte - 127.0)
    codes = (blocks / scale).astype(np.float32).astype(dtype).astype(np.float64)
    return np.moveaxis((codes * scale).reshape(v.shape), -1, axis)


WIDE = False


def mx_kscale(k):
    if not WIDE:
        return np.ones(k)
    levels = np.array([10, -10, 5, -5, 0])
    a = np.random.permutation(np.resize(levels, k // 512 * 4)).reshape(k // 512, 4)
    idx = np.arange(k)
    return np.exp2(a[idx // 512, idx % 128 // 32])


BF16 = ml_dtypes.bfloat16


def bf(x):
    return np.asarray(x, np.float32).astype(BF16)


def f64(x):
    return np.asarray(x).astype(np.float64)


E2M1 = np.array([0.0, 0.5, 1.0, 1.5, 2.0, 3.0, 4.0, 6.0, -0.0, -0.5, -1.0, -1.5, -2.0, -3.0, -4.0, -6.0])


def pack_weight(w, fmt):
    k, n = w.shape
    w = f64(bf(w)).reshape(k // 32, 32, n)
    amax = np.abs(w).max(1)
    if fmt == "e4m3":
        byte = np.frexp(amax)[1] - 1 + 127 - 7
    else:
        mant, ex = np.frexp(amax / 6.0)
        byte = np.where(mant > 0.5, ex, ex - 1) + 127
    byte = np.clip(np.where(amax > 0, byte, 1), 1, 254)
    scaled = (w * np.exp2(127.0 - byte)[:, None, :]).reshape(k, n).astype(np.float32)
    by_word = np.ascontiguousarray(scaled.reshape(k // 512, 128, 4, n).transpose(0, 1, 3, 2))
    if fmt == "e4m3":
        words = by_word.astype(ml_dtypes.float8_e4m3fn).view(np.uint8)
    else:
        c = by_word.astype(ml_dtypes.float4_e2m1fn).view(np.uint8) & 0xF
        words = c[..., 0::2] | (c[..., 1::2] << 4)
    return np.ascontiguousarray(words), np.ascontiguousarray(byte.astype(np.uint8).reshape(k // 512, 16, n))


def unpack_weight(words, scales, fmt):
    g, p, n, _ = words.shape
    if fmt == "e4m3":
        vals = np.ascontiguousarray(words).view(ml_dtypes.float8_e4m3fn).astype(np.float64)
    else:
        nib = np.empty((g, p, n, 4), np.uint8)
        nib[..., 0::2] = words & 0xF
        nib[..., 1::2] = words >> 4
        vals = E2M1[nib]
    vals = vals * np.repeat(np.exp2(scales.astype(np.float64) - 127.0), 8, axis=1)[..., None]
    return vals.transpose(0, 1, 3, 2).reshape(g * 512, n)


N, K, F, NB = 1024, 512, 384, 32
EPS = 1e-6
FMT = "e4m3"


def erf(v):
    a = np.minimum(np.abs(v), 6.0)
    term = a.copy()
    total = a.copy()
    for n in range(1, 130):
        term = term * (2.0 * a * a / (2.0 * n + 1.0))
        total = total + term
    return np.sign(v) * (2.0 / np.sqrt(np.pi)) * np.exp(-a * a) * total


def gelu(v):
    return 0.5 * v * (1.0 + erf(v / np.sqrt(2.0)))


def setup_inputs():
    s = mx_kscale(K)
    edge = np.random.random_sample((N, N)) < NB / N
    x = bf(np.random.standard_normal((N, K)) * s)
    adj = bf(np.random.random_sample((N, N)) * edge)
    W1_words, W1_scales = pack_weight(np.random.standard_normal((K, F)) * 3.0 / np.sqrt(K) / s[:, None], FMT)
    return {"x": x,
            "adj": adj,
            "W1_words": W1_words,
            "W1_scales": W1_scales,
            "b1": bf(np.random.standard_normal(F) * 0.3),
            "ln_gamma": bf(1.0 + 0.1 * np.random.standard_normal(F)),
            "ln_beta": bf(0.1 * np.random.standard_normal(F))}


def reference(x, adj, W1_words, W1_scales, b1, ln_gamma, ln_beta):
    a = f64(adj)
    h = (mxq(f64(x), 1, "e4m3") @ unpack_weight(W1_words, W1_scales, FMT)) + f64(b1)
    deg = a.sum(axis=1) + 1.0
    dinv = np.where(deg > 0, deg ** -0.5, 0.0)
    hs = dinv[:, None] * h
    agg = (mxq(a, 1, "e4m3") @ mxq(hs, 0, "e4m3")) + hs
    g = gelu(dinv[:, None] * agg)
    mu = g.mean(axis=-1, keepdims=True)
    var = ((g - mu) ** 2).mean(axis=-1, keepdims=True)
    return (g - mu) / np.sqrt(var + EPS) * f64(ln_gamma) + f64(ln_beta)

@@ -1,0 +1,249 @@
+import concourse.mybir as mybir
+from concourse.masks import make_identity
+
+F32 = mybir.dt.float32
+BF16 = mybir.dt.bfloat16
+I32 = mybir.dt.int32
+U32 = mybir.dt.uint32
+U8 = mybir.dt.uint8
+FP8X4 = mybir.dt.float8_e4m3fn_x4
+ALU = mybir.AluOpType
+ACT = mybir.ActivationFunctionType
+
+P = 128
+PACK = 4
+NODES = 1024
+K_IN = 512
+FEAT = 384
+EPS = 1e-6
+BLOCKS = NODES // P
+PASSES = NODES // (P * PACK)
+CHUNKS = BLOCKS // 2
+BANK = 512
+FEAT_CUTS = ((0, 256), (256, 128))
+
+FLOPS = 2 * NODES * K_IN * FEAT + 2 * NODES * NODES * FEAT
+
+
+def tile_gcnlayer_pa_kernel(tc, x, adj, W1_words, W1_scales, b1, ln_gamma, ln_beta, out):
+    nc = tc.nc
+
+    x_view = x.rearrange("(q p e) k -> p q e k", q=CHUNKS, p=P, e=2)
+    adj_view = adj.rearrange("(q p e) j -> p q e j", q=CHUNKS, p=P, e=2)
+    out_view = out.rearrange("(q p e) f -> p q e f", q=CHUNKS, p=P, e=2)
+
+    with tc.tile_pool(name="keep", bufs=1) as keep, tc.psum_pool(name="turn", bufs=3) as turn, tc.psum_pool(
+        name="acc", bufs=4
+    ) as acc:
+        x_sb = keep.tile([P, BLOCKS, K_IN], BF16)
+        adj_sb = keep.tile([P, BLOCKS, NODES], BF16)
+        w_codes = keep.tile([P, FEAT], U32, align_bytes=64)
+        w_scales = keep.tile([P, FEAT], U8, align_bytes=64)
+
+        x_grouped = keep.tile([P, BLOCKS, P, PACK], BF16, align_bytes=64)
+        x_codes = keep.tile([P, BLOCKS, P], U32, align_bytes=64)
+        x_scales = keep.tile([P, BLOCKS, P], U8, align_bytes=64)
+        adj_grouped = keep.tile([P, BLOCKS, PASSES, P, PACK], BF16, align_bytes=64)
+        adj_codes = keep.tile([P, BLOCKS, PASSES, P], U32, align_bytes=64)
+        adj_scales = keep.tile([P, BLOCKS, PASSES, P], U8, align_bytes=64)
+        hs_grouped = keep.tile([P, PASSES, FEAT, PACK], BF16, align_bytes=64)
+        hs_codes = keep.tile([P, PASSES, FEAT], U32, align_bytes=64)
+        hs_scales = keep.tile([P, PASSES, FEAT], U8, align_bytes=64)
+
+        identity = keep.tile([P, P], F32)
+        ones = keep.tile([P, P], BF16)
+        vector_rows = keep.tile([P, 3, BANK], BF16)
+        b1_all = keep.tile([P, FEAT], F32)
+        gamma_all = keep.tile([P, FEAT], F32)
+        beta_all = keep.tile([P, FEAT], F32)
+        minus_half = keep.tile([P, 2], F32)
+        table_in = keep.tile([P, 1], F32)
+        table_out = keep.tile([P, 1], F32)
+
+        pair_sums = keep.tile([P, BLOCKS, NODES // 2], F32)
+        row_sum = keep.tile([P, BLOCKS], F32)
+        deg = keep.tile([P, BLOCKS], F32)
+        dinv = keep.tile([P, BLOCKS], F32)
+
+        h_bias = keep.tile([P, BLOCKS, FEAT], F32)
+        pre = keep.tile([P, BLOCKS, FEAT], F32)
+        g = keep.tile([P, BLOCKS, FEAT], F32)
+        squares = keep.tile([P, BLOCKS, FEAT], F32)
+        scaled = keep.tile([P, BLOCKS, FEAT], F32)
+        result = keep.tile([P, BLOCKS, FEAT], F32)
+        g_sum = keep.tile([P, BLOCKS], F32)
+        minus_mean = keep.tile([P, BLOCKS], F32)
+        square_sum = keep.tile([P, BLOCKS], F32)
+        var_eps = keep.tile([P, BLOCKS], F32)
+        rstd = keep.tile([P, BLOCKS], F32)
+
+        nc.vector.memset(w_scales[:].bitcast(I32), 0)
+        nc.vector.memset(vector_rows[:], 0.0)
+        nc.vector.memset(ones[:], 1.0)
+        nc.vector.memset(minus_half[:], -0.5)
+        nc.vector.memset(table_in[:], 0.0)
+        make_identity(nc, identity[:])
+        nc.scalar.activation(out=table_out[:], in_=table_in[:], func=ACT.Gelu)
+
+        for v, vector in enumerate((b1, ln_gamma, ln_beta)):
+            nc.scalar.dma_start(out=vector_rows[0:1, v, 0:FEAT], in_=vector.unsqueeze(0))
+        for c in range(PASSES):
+            nc.sync.dma_start(
+                out=x_sb[:, 4 * c : 4 * c + 4, :].rearrange("p (q e) k -> p q e k", e=2),
+                in_=x_view[:, 2 * c : 2 * c + 2, :, :],
+            )
+        nc.sync.dma_start(
+            out=w_codes[:].bitcast(I32), in_=W1_words.rearrange("g p n t -> (g p) (n t)").bitcast(I32)
+        )
+        for quadrant in range(4):
+            nc.sync.dma_start(
+                out=w_scales[32 * quadrant : 32 * quadrant + 4, :].bitcast(I32),
+                in_=W1_scales[0, 4 * quadrant : 4 * quadrant + 4, :].bitcast(I32),
+            )
+        for q in range(CHUNKS):
+            nc.sync.dma_start(out=adj_sb[:, 2 * q : 2 * q + 2, :], in_=adj_view[:, q, :, :])
+
+        for v, spread in enumerate((b1_all, gamma_all, beta_all)):
+            spread_ps = acc.tile([P, BANK], F32, tag="acc")
+            nc.tensor.matmul(out=spread_ps[:], lhsT=ones[:], rhs=vector_rows[:, v, :], start=True, stop=True)
+            nc.scalar.copy(out=spread[:], in_=spread_ps[:, 0:FEAT])
+
+        for pair in range(BLOCKS // 2):
+            x_turned = turn.tile([P, 2, 2, P], F32, tag="turn")
+            for i in range(2):
+                x_words = x_sb[:, 2 * pair + i, :].bitcast(F32)
+                for u in range(2):
+                    nc.tensor.transpose(
+                        out=x_turned[:, i, u, :], in_=x_words[:, u : K_IN // 2 : 2], identity=identity[:]
+                    )
+            both = slice(2 * pair, 2 * pair + 2)
+            nc.scalar.copy(
+                out=x_grouped[:, both, :, :].bitcast(F32), in_=x_turned[:].rearrange("p i u n -> p i n u")
+            )
+            nc.vector.quantize_mx(
+                out=x_codes[:, both, :].rearrange("p i n -> p (i n)").bitcast(FP8X4),
+                scales=x_scales[:, both, :].rearrange("p i n -> p (i n)"),
+                in_=x_grouped[:, both, :, :].rearrange("p i n t -> p (i n t)"),
+            )
+            for b in range(2 * pair, 2 * pair + 2):
+                h_ps = acc.tile([P, FEAT], F32, tag="acc")
+                for f0, width in FEAT_CUTS:
+                    nc.tensor.matmul_mx(
+                        out=h_ps[:, f0 : f0 + width],
+                        lhsT=x_codes[:, b, :].bitcast(FP8X4),
+                        lhsT_scale=x_scales[:, b, :],
+                        rhs=w_codes[:, f0 : f0 + width].bitcast(FP8X4),
+                        rhs_scale=w_scales[:, f0 : f0 + width],
+                        start=True,
+                        stop=True,
+                    )
+                nc.vector.tensor_tensor(out=h_bias[:, b, :], in0=h_ps[:], in1=b1_all[:], op=ALU.add)
+
+        for q in range(CHUNKS):
+            both = slice(2 * q, 2 * q + 2)
+            for b in range(2 * q, 2 * q + 2):
+                nc.vector.scalar_tensor_tensor(
+                    out=pair_sums[:, b, :],
+                    in0=adj_sb[:, b, 0 : NODES // 2],
+                    scalar=1.0,
+                    in1=adj_sb[:, b, NODES // 2 : NODES],
+                    op0=ALU.mult,
+                    op1=ALU.add,
+                    accum_out=row_sum[:, b : b + 1],
+                )
+            nc.gpsimd.tensor_scalar(
+                out=deg[:, both], in0=row_sum[:, both], scalar1=1.0, scalar2=1.0, op0=ALU.mult, op1=ALU.add
+            )
+            nc.gpsimd.tensor_tensor(out=dinv[:, both], in0=deg[:, both], in1=minus_half[:], op=ALU.pow)
+
+            for b in range(2 * q, 2 * q + 2):
+                adj_words = adj_sb[:, b, :].bitcast(F32)
+                adj_turned = turn.tile([P, PASSES, 2, P], F32, tag="turn")
+                for c in range(PASSES):
+                    for u in range(2):
+                        first = (2 * c + u) * P
+                        nc.tensor.transpose(
+                            out=adj_turned[:, c, u, :], in_=adj_words[:, first : first + P], identity=identity[:]
+                        )
+                nc.scalar.copy(
+                    out=adj_grouped[:, b, :, :, :].bitcast(F32),
+                    in_=adj_turned[:].rearrange("p c u i -> p c i u"),
+                )
+                nc.vector.quantize_mx(
+                    out=adj_codes[:, b, :, :].rearrange("p c i -> p (c i)").bitcast(FP8X4),
+                    scales=adj_scales[:, b, :, :].rearrange("p c i -> p (c i)"),
+                    in_=adj_grouped[:, b, :, :, :].rearrange("p c i t -> p (c i t)"),
+                )
+
+            if q % 2 == 1:
+                c = q // 2
+                four = slice(4 * c, 4 * c + 4)
+                nc.vector.tensor_tensor(
+                    out=hs_grouped[:, c, :, :],
+                    in0=h_bias[:, four, :].rearrange("p t f -> p f t"),
+                    in1=dinv[:, four].unsqueeze(1).to_broadcast([P, FEAT, PACK]),
+                    op=ALU.mult,
+                )
+                for f0, width in FEAT_CUTS:
+                    nc.vector.quantize_mx(
+                        out=hs_codes[:, c, f0 : f0 + width].bitcast(FP8X4),
+                        scales=hs_scales[:, c, f0 : f0 + width],
+                        in_=hs_grouped[:, c, f0 : f0 + width, :].rearrange("p f t -> p (f t)"),
+                    )
+
+        for b in range(BLOCKS):
+            one = slice(b, b + 1)
+            agg_ps = acc.tile([P, FEAT], F32, tag="acc")
+            for f0, width in FEAT_CUTS:
+                for c in range(PASSES):
+                    nc.tensor.matmul_mx(
+                        out=agg_ps[:, f0 : f0 + width],
+                        lhsT=adj_codes[:, b, c, :].bitcast(FP8X4),
+                        lhsT_scale=adj_scales[:, b, c, :],
+                        rhs=hs_codes[:, c, f0 : f0 + width].bitcast(FP8X4),
+                        rhs_scale=hs_scales[:, c, f0 : f0 + width],
+                        start=(c == 0),
+                        stop=(c == PASSES - 1),
+                    )
+            nc.vector.scalar_tensor_tensor(
+                out=pre[:, b, :],
+                in0=h_bias[:, b, :],
+                scalar=dinv[:, one],
+                in1=agg_ps[:],
+                op0=ALU.mult,
+                op1=ALU.add,
+            )
+            nc.scalar.activation(
+                out=g[:, b, :], in_=pre[:, b, :], func=ACT.Gelu, scale=dinv[:, one], accum_out=g_sum[:, one]
+            )
+            nc.gpsimd.tensor_scalar(
+                out=minus_mean[:, one], in0=g_sum[:, one], scalar1=-1.0 / FEAT, scalar2=0.0, op0=ALU.mult, op1=ALU.add
+            )
+            nc.scalar.activation(
+                out=squares[:, b, :],
+                in_=g[:, b, :],
+                func=ACT.Square,
+                bias=minus_mean[:, one],
+                accum_out=square_sum[:, one],
+            )
+            nc.vector.scalar_tensor_tensor(
+                out=scaled[:, b, :],
+                in0=g[:, b, :],
+                scalar=minus_mean[:, one],
+                in1=gamma_all[:],
+                op0=ALU.add,
+                op1=ALU.mult,
+            )
+            nc.gpsimd.tensor_scalar(
+                out=var_eps[:, one], in0=square_sum[:, one], scalar1=1.0 / FEAT, scalar2=EPS, op0=ALU.mult, op1=ALU.add
+            )
+            nc.gpsimd.tensor_tensor(out=rstd[:, one], in0=var_eps[:, one], in1=minus_half[:, 0:1], op=ALU.pow)
+            nc.vector.scalar_tensor_tensor(
+                out=result[:, b, :],
+                in0=scaled[:, b, :],
+                scalar=rstd[:, one],
+                in1=beta_all[:],
+                op0=ALU.mult,
+                op1=ALU.add,
+            )
+            nc.sync.dma_start(out=out_view[:, b // 2, b % 2, :], in_=result[:, b, :])

@@ -21,6 +21,8 @@ PASSES = NODES // (P * PACK)
 CHUNKS = BLOCKS // 2
 BANK = 512
 FEAT_CUTS = ((0, 256), (256, 128))
+SELF_LOOP = 16
+ROW = NODES + SELF_LOOP
 
 FLOPS = 2 * NODES * K_IN * FEAT + 2 * NODES * NODES * FEAT
 
@@ -32,11 +34,11 @@ def tile_gcnlayer_pa_kernel(tc, x, adj, W1_words, W1_scales, b1, ln_gamma, ln_be
     adj_view = adj.rearrange("(q p e) j -> p q e j", q=CHUNKS, p=P, e=2)
     out_view = out.rearrange("(q p e) f -> p q e f", q=CHUNKS, p=P, e=2)
 
-    with tc.tile_pool(name="keep", bufs=1) as keep, tc.psum_pool(name="turn", bufs=3) as turn, tc.psum_pool(
-        name="acc", bufs=4
-    ) as acc:
+    with tc.manual_schedule(), tc.tile_pool(name="keep", bufs=1) as keep, tc.psum_pool(
+        name="turn", bufs=4
+    ) as turn, tc.psum_pool(name="acc", bufs=4) as acc:
         x_sb = keep.tile([P, BLOCKS, K_IN], BF16)
-        adj_sb = keep.tile([P, BLOCKS, NODES], BF16)
+        adj_sb = keep.tile([P, BLOCKS, ROW], BF16)
         w_codes = keep.tile([P, FEAT], U32, align_bytes=64)
         w_scales = keep.tile([P, FEAT], U8, align_bytes=64)
 
@@ -60,9 +62,10 @@ def tile_gcnlayer_pa_kernel(tc, x, adj, W1_words, W1_scales, b1, ln_gamma, ln_be
         table_in = keep.tile([P, 1], F32)
         table_out = keep.tile([P, 1], F32)
 
-        pair_sums = keep.tile([P, BLOCKS, NODES // 2], F32)
-        row_sum = keep.tile([P, BLOCKS], F32)
-        deg = keep.tile([P, BLOCKS], F32)
+        pair_sums = keep.tile([P, PASSES, 2, ROW // 2], F32)
+        row_copy = keep.tile([P, PASSES, 2, ROW], BF16)
+        deg_scalar = keep.tile([P, PASSES, 2], F32)
+        deg_vector = keep.tile([P, PASSES, 2], F32)
         dinv = keep.tile([P, BLOCKS], F32)
 
         h_bias = keep.tile([P, BLOCKS, FEAT], F32)
@@ -77,122 +80,103 @@ def tile_gcnlayer_pa_kernel(tc, x, adj, W1_words, W1_scales, b1, ln_gamma, ln_be
         var_eps = keep.tile([P, BLOCKS], F32)
         rstd = keep.tile([P, BLOCKS], F32)
 
-        nc.vector.memset(w_scales[:].bitcast(I32), 0)
-        nc.vector.memset(vector_rows[:], 0.0)
-        nc.vector.memset(ones[:], 1.0)
-        nc.vector.memset(minus_half[:], -0.5)
-        nc.vector.memset(table_in[:], 0.0)
-        make_identity(nc, identity[:])
-        nc.scalar.activation(out=table_out[:], in_=table_in[:], func=ACT.Gelu)
-
-        for v, vector in enumerate((b1, ln_gamma, ln_beta)):
-            nc.scalar.dma_start(out=vector_rows[0:1, v, 0:FEAT], in_=vector.unsqueeze(0))
-        for c in range(PASSES):
-            nc.sync.dma_start(
-                out=x_sb[:, 4 * c : 4 * c + 4, :].rearrange("p (q e) k -> p q e k", e=2),
-                in_=x_view[:, 2 * c : 2 * c + 2, :, :],
-            )
-        nc.sync.dma_start(
-            out=w_codes[:].bitcast(I32), in_=W1_words.rearrange("g p n t -> (g p) (n t)").bitcast(I32)
-        )
-        for quadrant in range(4):
-            nc.sync.dma_start(
-                out=w_scales[32 * quadrant : 32 * quadrant + 4, :].bitcast(I32),
-                in_=W1_scales[0, 4 * quadrant : 4 * quadrant + 4, :].bitcast(I32),
-            )
-        for q in range(CHUNKS):
-            nc.sync.dma_start(out=adj_sb[:, 2 * q : 2 * q + 2, :], in_=adj_view[:, q, :, :])
-
-        for v, spread in enumerate((b1_all, gamma_all, beta_all)):
+        def spread(v, everywhere):
             spread_ps = acc.tile([P, BANK], F32, tag="acc")
             nc.tensor.matmul(out=spread_ps[:], lhsT=ones[:], rhs=vector_rows[:, v, :], start=True, stop=True)
-            nc.scalar.copy(out=spread[:], in_=spread_ps[:, 0:FEAT])
+            nc.scalar.copy(out=everywhere[:], in_=spread_ps[:, 0:FEAT])
 
-        for pair in range(BLOCKS // 2):
+        def turn_x(q):
             x_turned = turn.tile([P, 2, 2, P], F32, tag="turn")
-            for i in range(2):
-                x_words = x_sb[:, 2 * pair + i, :].bitcast(F32)
+            for e in range(2):
+                x_words = x_sb[:, 2 * q + e, :].bitcast(F32)
                 for u in range(2):
                     nc.tensor.transpose(
-                        out=x_turned[:, i, u, :], in_=x_words[:, u : K_IN // 2 : 2], identity=identity[:]
+                        out=x_turned[:, e, u, :], in_=x_words[:, u : K_IN // 2 : 2], identity=identity[:]
                     )
-            both = slice(2 * pair, 2 * pair + 2)
             nc.scalar.copy(
-                out=x_grouped[:, both, :, :].bitcast(F32), in_=x_turned[:].rearrange("p i u n -> p i n u")
+                out=x_grouped[:, 2 * q : 2 * q + 2, :, :].bitcast(F32),
+                in_=x_turned[:].rearrange("p e u n -> p e n u"),
             )
-            nc.vector.quantize_mx(
-                out=x_codes[:, both, :].rearrange("p i n -> p (i n)").bitcast(FP8X4),
-                scales=x_scales[:, both, :].rearrange("p i n -> p (i n)"),
-                in_=x_grouped[:, both, :, :].rearrange("p i n t -> p (i n t)"),
-            )
-            for b in range(2 * pair, 2 * pair + 2):
-                h_ps = acc.tile([P, FEAT], F32, tag="acc")
-                for f0, width in FEAT_CUTS:
-                    nc.tensor.matmul_mx(
-                        out=h_ps[:, f0 : f0 + width],
-                        lhsT=x_codes[:, b, :].bitcast(FP8X4),
-                        lhsT_scale=x_scales[:, b, :],
-                        rhs=w_codes[:, f0 : f0 + width].bitcast(FP8X4),
-                        rhs_scale=w_scales[:, f0 : f0 + width],
-                        start=True,
-                        stop=True,
-                    )
-                nc.vector.tensor_tensor(out=h_bias[:, b, :], in0=h_ps[:], in1=b1_all[:], op=ALU.add)
 
-        for q in range(CHUNKS):
+        def quantise_x(q):
             both = slice(2 * q, 2 * q + 2)
-            for b in range(2 * q, 2 * q + 2):
-                nc.vector.scalar_tensor_tensor(
-                    out=pair_sums[:, b, :],
-                    in0=adj_sb[:, b, 0 : NODES // 2],
-                    scalar=1.0,
-                    in1=adj_sb[:, b, NODES // 2 : NODES],
-                    op0=ALU.mult,
-                    op1=ALU.add,
-                    accum_out=row_sum[:, b : b + 1],
-                )
-            nc.gpsimd.tensor_scalar(
-                out=deg[:, both], in0=row_sum[:, both], scalar1=1.0, scalar2=1.0, op0=ALU.mult, op1=ALU.add
+            nc.vector.quantize_mx(
+                out=x_codes[:, both, :].rearrange("p e n -> p (e n)").bitcast(FP8X4),
+                scales=x_scales[:, both, :].rearrange("p e n -> p (e n)"),
+                in_=x_grouped[:, both, :, :].rearrange("p e n t -> p (e n t)"),
             )
-            nc.gpsimd.tensor_tensor(out=dinv[:, both], in0=deg[:, both], in1=minus_half[:], op=ALU.pow)
 
-            for b in range(2 * q, 2 * q + 2):
-                adj_words = adj_sb[:, b, :].bitcast(F32)
-                adj_turned = turn.tile([P, PASSES, 2, P], F32, tag="turn")
-                for c in range(PASSES):
-                    for u in range(2):
-                        first = (2 * c + u) * P
-                        nc.tensor.transpose(
-                            out=adj_turned[:, c, u, :], in_=adj_words[:, first : first + P], identity=identity[:]
-                        )
-                nc.scalar.copy(
-                    out=adj_grouped[:, b, :, :, :].bitcast(F32),
-                    in_=adj_turned[:].rearrange("p c u i -> p c i u"),
+        def first_product(b):
+            h_ps = acc.tile([P, FEAT], F32, tag="acc")
+            for f0, width in FEAT_CUTS:
+                nc.tensor.matmul_mx(
+                    out=h_ps[:, f0 : f0 + width],
+                    lhsT=x_codes[:, b, :].bitcast(FP8X4),
+                    lhsT_scale=x_scales[:, b, :],
+                    rhs=w_codes[:, f0 : f0 + width].bitcast(FP8X4),
+                    rhs_scale=w_scales[:, f0 : f0 + width],
+                    start=True,
+                    stop=True,
                 )
-                nc.vector.quantize_mx(
-                    out=adj_codes[:, b, :, :].rearrange("p c i -> p (c i)").bitcast(FP8X4),
-                    scales=adj_scales[:, b, :, :].rearrange("p c i -> p (c i)"),
-                    in_=adj_grouped[:, b, :, :, :].rearrange("p c i t -> p (c i t)"),
-                )
+            nc.vector.tensor_tensor(out=h_bias[:, b, :], in0=h_ps[:], in1=b1_all[:], op=ALU.add)
 
-            if q % 2 == 1:
-                c = q // 2
-                four = slice(4 * c, 4 * c + 4)
-                nc.vector.tensor_tensor(
-                    out=hs_grouped[:, c, :, :],
-                    in0=h_bias[:, four, :].rearrange("p t f -> p f t"),
-                    in1=dinv[:, four].unsqueeze(1).to_broadcast([P, FEAT, PACK]),
-                    op=ALU.mult,
-                )
-                for f0, width in FEAT_CUTS:
-                    nc.vector.quantize_mx(
-                        out=hs_codes[:, c, f0 : f0 + width].bitcast(FP8X4),
-                        scales=hs_scales[:, c, f0 : f0 + width],
-                        in_=hs_grouped[:, c, f0 : f0 + width, :].rearrange("p f t -> p (f t)"),
+        def degrees(q):
+            c, u = divmod(q, 2)
+            for e in range(2):
+                row = adj_sb[:, 2 * q + e, :]
+                if u == 0:
+                    nc.scalar.activation(
+                        out=row_copy[:, c, e, :], in_=row, func=ACT.Copy, accum_out=deg_scalar[:, c, e : e + 1]
                     )
+                else:
+                    nc.vector.scalar_tensor_tensor(
+                        out=pair_sums[:, c, e, :],
+                        in0=row[:, 0 : ROW // 2],
+                        scalar=1.0,
+                        in1=row[:, ROW // 2 : ROW],
+                        op0=ALU.mult,
+                        op1=ALU.add,
+                        accum_out=deg_vector[:, c, e : e + 1],
+                    )
+            deg = deg_scalar if u == 0 else deg_vector
+            nc.gpsimd.tensor_tensor(out=dinv[:, 2 * q : 2 * q + 2], in0=deg[:, c, :], in1=minus_half[:], op=ALU.pow)
 
-        for b in range(BLOCKS):
-            one = slice(b, b + 1)
+        def turn_adj(b):
+            adj_words = adj_sb[:, b, 0:NODES].bitcast(F32)
+            adj_turned = turn.tile([P, PASSES, 2, P], F32, tag="turn")
+            for c in range(PASSES):
+                for u in range(2):
+                    first = (2 * c + u) * P
+                    nc.tensor.transpose(
+                        out=adj_turned[:, c, u, :], in_=adj_words[:, first : first + P], identity=identity[:]
+                    )
+            nc.scalar.copy(
+                out=adj_grouped[:, b, :, :, :].bitcast(F32), in_=adj_turned[:].rearrange("p c u i -> p c i u")
+            )
+
+        def quantise_adj(b):
+            nc.vector.quantize_mx(
+                out=adj_codes[:, b, :, :].rearrange("p c i -> p (c i)").bitcast(FP8X4),
+                scales=adj_scales[:, b, :, :].rearrange("p c i -> p (c i)"),
+                in_=adj_grouped[:, b, :, :, :].rearrange("p c i t -> p (c i t)"),
+            )
+
+        def make_hs(c):
+            four = slice(4 * c, 4 * c + 4)
+            nc.vector.tensor_tensor(
+                out=hs_grouped[:, c, :, :],
+                in0=h_bias[:, four, :].rearrange("p t f -> p f t"),
+                in1=dinv[:, four].unsqueeze(1).to_broadcast([P, FEAT, PACK]),
+                op=ALU.mult,
+            )
+            for f0, width in FEAT_CUTS:
+                nc.vector.quantize_mx(
+                    out=hs_codes[:, c, f0 : f0 + width].bitcast(FP8X4),
+                    scales=hs_scales[:, c, f0 : f0 + width],
+                    in_=hs_grouped[:, c, f0 : f0 + width, :].rearrange("p f t -> p (f t)"),
+                )
+
+        def second_product(b):
             agg_ps = acc.tile([P, FEAT], F32, tag="acc")
             for f0, width in FEAT_CUTS:
                 for c in range(PASSES):
@@ -208,17 +192,23 @@ def tile_gcnlayer_pa_kernel(tc, x, adj, W1_words, W1_scales, b1, ln_gamma, ln_be
             nc.vector.scalar_tensor_tensor(
                 out=pre[:, b, :],
                 in0=h_bias[:, b, :],
-                scalar=dinv[:, one],
+                scalar=dinv[:, b : b + 1],
                 in1=agg_ps[:],
                 op0=ALU.mult,
                 op1=ALU.add,
             )
+
+        def gelu_and_mean(b):
+            one = slice(b, b + 1)
             nc.scalar.activation(
                 out=g[:, b, :], in_=pre[:, b, :], func=ACT.Gelu, scale=dinv[:, one], accum_out=g_sum[:, one]
             )
             nc.gpsimd.tensor_scalar(
                 out=minus_mean[:, one], in0=g_sum[:, one], scalar1=-1.0 / FEAT, scalar2=0.0, op0=ALU.mult, op1=ALU.add
             )
+
+        def variance(b):
+            one = slice(b, b + 1)
             nc.scalar.activation(
                 out=squares[:, b, :],
                 in_=g[:, b, :],
@@ -226,24 +216,85 @@ def tile_gcnlayer_pa_kernel(tc, x, adj, W1_words, W1_scales, b1, ln_gamma, ln_be
                 bias=minus_mean[:, one],
                 accum_out=square_sum[:, one],
             )
-            nc.vector.scalar_tensor_tensor(
-                out=scaled[:, b, :],
-                in0=g[:, b, :],
-                scalar=minus_mean[:, one],
-                in1=gamma_all[:],
-                op0=ALU.add,
-                op1=ALU.mult,
-            )
             nc.gpsimd.tensor_scalar(
                 out=var_eps[:, one], in0=square_sum[:, one], scalar1=1.0 / FEAT, scalar2=EPS, op0=ALU.mult, op1=ALU.add
             )
             nc.gpsimd.tensor_tensor(out=rstd[:, one], in0=var_eps[:, one], in1=minus_half[:, 0:1], op=ALU.pow)
+
+        def centre_and_gain(b):
+            nc.vector.scalar_tensor_tensor(
+                out=scaled[:, b, :],
+                in0=g[:, b, :],
+                scalar=minus_mean[:, b : b + 1],
+                in1=gamma_all[:],
+                op0=ALU.add,
+                op1=ALU.mult,
+            )
+
+        def finish(b):
             nc.vector.scalar_tensor_tensor(
                 out=result[:, b, :],
                 in0=scaled[:, b, :],
-                scalar=rstd[:, one],
+                scalar=rstd[:, b : b + 1],
                 in1=beta_all[:],
                 op0=ALU.mult,
                 op1=ALU.add,
             )
             nc.sync.dma_start(out=out_view[:, b // 2, b % 2, :], in_=result[:, b, :])
+
+        nc.vector.memset(w_scales[:].bitcast(I32), 0)
+        nc.vector.memset(vector_rows[:], 0.0)
+        nc.vector.memset(ones[:], 1.0)
+        nc.vector.memset(minus_half[:], -0.5)
+        nc.vector.memset(table_in[:], 0.0)
+        nc.vector.memset(adj_sb[:, :, NODES:ROW], 0.0)
+        nc.vector.memset(adj_sb[:, :, NODES : NODES + 1], 1.0)
+        make_identity(nc, identity[:])
+        nc.scalar.activation(out=table_out[:], in_=table_in[:], func=ACT.Gelu)
+
+        for v, vector in enumerate((b1, ln_gamma, ln_beta)):
+            nc.gpsimd.dma_start(out=vector_rows[0:1, v, 0:FEAT], in_=vector.unsqueeze(0))
+        for q in range(2):
+            nc.sync.dma_start(out=x_sb[:, 2 * q : 2 * q + 2, :], in_=x_view[:, q, :, :])
+        nc.sync.dma_start(
+            out=w_codes[:].bitcast(I32), in_=W1_words.rearrange("g p n t -> (g p) (n t)").bitcast(I32)
+        )
+        for quadrant in range(4):
+            nc.sync.dma_start(
+                out=w_scales[32 * quadrant : 32 * quadrant + 4, :].bitcast(I32),
+                in_=W1_scales[0, 4 * quadrant : 4 * quadrant + 4, :].bitcast(I32),
+            )
+        for q in range(2, CHUNKS):
+            nc.sync.dma_start(out=x_sb[:, 2 * q : 2 * q + 2, :], in_=x_view[:, q, :, :])
+        for q in range(CHUNKS):
+            nc.sync.dma_start(out=adj_sb[:, 2 * q : 2 * q + 2, 0:NODES], in_=adj_view[:, q, :, :])
+
+        spread(0, b1_all)
+        for q in range(CHUNKS):
+            turn_x(q)
+        for half in range(2):
+            quantise_x(2 * half)
+            quantise_x(2 * half + 1)
+            for b in range(4 * half, 4 * half + 4):
+                first_product(b)
+        spread(1, gamma_all)
+        spread(2, beta_all)
+
+        for q in range(CHUNKS):
+            degrees(q)
+            turn_adj(2 * q)
+            turn_adj(2 * q + 1)
+            quantise_adj(2 * q)
+            quantise_adj(2 * q + 1)
+            if q % 2 == 1:
+                make_hs(q // 2)
+
+        for s in range(BLOCKS + 3):
+            if s < BLOCKS:
+                second_product(s)
+                gelu_and_mean(s)
+            if 3 <= s:
+                finish(s - 3)
+            if 1 <= s <= BLOCKS:
+                variance(s - 1)
+                centre_and_gain(s - 1)

@@ -35,8 +35,8 @@ def tile_gcnlayer_pa_kernel(tc, x, adj, W1_words, W1_scales, b1, ln_gamma, ln_be
     out_view = out.rearrange("(q p e) f -> p q e f", q=CHUNKS, p=P, e=2)
 
     with tc.manual_schedule(), tc.tile_pool(name="keep", bufs=1) as keep, tc.psum_pool(
-        name="turn", bufs=4
-    ) as turn, tc.psum_pool(name="acc", bufs=4) as acc:
+        name="fixed", bufs=1
+    ) as fixed, tc.psum_pool(name="turn", bufs=3) as turn, tc.psum_pool(name="acc", bufs=4) as acc:
         x_sb = keep.tile([P, BLOCKS, K_IN], BF16)
         adj_sb = keep.tile([P, BLOCKS, ROW], BF16)
         w_codes = keep.tile([P, FEAT], U32, align_bytes=64)
@@ -56,8 +56,7 @@ def tile_gcnlayer_pa_kernel(tc, x, adj, W1_words, W1_scales, b1, ln_gamma, ln_be
         ones = keep.tile([P, P], BF16)
         vector_rows = keep.tile([P, 3, BANK], BF16)
         b1_all = keep.tile([P, FEAT], F32)
-        gamma_all = keep.tile([P, FEAT], F32)
-        beta_all = keep.tile([P, FEAT], F32)
+        gamma_beta = fixed.tile([P, 2, BANK], BF16)
         minus_half = keep.tile([P, 2], F32)
         table_in = keep.tile([P, 1], F32)
         table_out = keep.tile([P, 1], F32)
@@ -81,9 +80,7 @@ def tile_gcnlayer_pa_kernel(tc, x, adj, W1_words, W1_scales, b1, ln_gamma, ln_be
         rstd = keep.tile([P, BLOCKS], F32)
 
         def spread(v, everywhere):
-            spread_ps = acc.tile([P, BANK], F32, tag="acc")
-            nc.tensor.matmul(out=spread_ps[:], lhsT=ones[:], rhs=vector_rows[:, v, :], start=True, stop=True)
-            nc.scalar.copy(out=everywhere[:], in_=spread_ps[:, 0:FEAT])
+            nc.tensor.matmul(out=everywhere, lhsT=ones[:], rhs=vector_rows[:, v, :], start=True, stop=True)
 
         def turn_x(q):
             x_turned = turn.tile([P, 2, 2, P], F32, tag="turn")
@@ -203,11 +200,9 @@ def tile_gcnlayer_pa_kernel(tc, x, adj, W1_words, W1_scales, b1, ln_gamma, ln_be
             nc.scalar.activation(
                 out=g[:, b, :], in_=pre[:, b, :], func=ACT.Gelu, scale=dinv[:, one], accum_out=g_sum[:, one]
             )
-            nc.gpsimd.tensor_scalar(
-                out=minus_mean[:, one], in0=g_sum[:, one], scalar1=-1.0 / FEAT, scalar2=0.0, op0=ALU.mult, op1=ALU.add
-            )
+            nc.scalar.mul(out=minus_mean[:, one], in_=g_sum[:, one], mul=-1.0 / FEAT)
 
-        def variance(b):
+        def sum_of_squares(b):
             one = slice(b, b + 1)
             nc.scalar.activation(
                 out=squares[:, b, :],
@@ -216,17 +211,20 @@ def tile_gcnlayer_pa_kernel(tc, x, adj, W1_words, W1_scales, b1, ln_gamma, ln_be
                 bias=minus_mean[:, one],
                 accum_out=square_sum[:, one],
             )
+
+        def inverse_std(q):
+            both = slice(2 * q, 2 * q + 2)
             nc.gpsimd.tensor_scalar(
-                out=var_eps[:, one], in0=square_sum[:, one], scalar1=1.0 / FEAT, scalar2=EPS, op0=ALU.mult, op1=ALU.add
+                out=var_eps[:, both], in0=square_sum[:, both], scalar1=1.0 / FEAT, scalar2=EPS, op0=ALU.mult, op1=ALU.add
             )
-            nc.gpsimd.tensor_tensor(out=rstd[:, one], in0=var_eps[:, one], in1=minus_half[:, 0:1], op=ALU.pow)
+            nc.gpsimd.tensor_tensor(out=rstd[:, both], in0=var_eps[:, both], in1=minus_half[:], op=ALU.pow)
 
         def centre_and_gain(b):
             nc.vector.scalar_tensor_tensor(
                 out=scaled[:, b, :],
                 in0=g[:, b, :],
                 scalar=minus_mean[:, b : b + 1],
-                in1=gamma_all[:],
+                in1=gamma_beta[:, 0, 0:FEAT],
                 op0=ALU.add,
                 op1=ALU.mult,
             )
@@ -236,7 +234,7 @@ def tile_gcnlayer_pa_kernel(tc, x, adj, W1_words, W1_scales, b1, ln_gamma, ln_be
                 out=result[:, b, :],
                 in0=scaled[:, b, :],
                 scalar=rstd[:, b : b + 1],
-                in1=beta_all[:],
+                in1=gamma_beta[:, 1, 0:FEAT],
                 op0=ALU.mult,
                 op1=ALU.add,
             )
@@ -250,10 +248,10 @@ def tile_gcnlayer_pa_kernel(tc, x, adj, W1_words, W1_scales, b1, ln_gamma, ln_be
         nc.vector.memset(adj_sb[:, :, NODES:ROW], 0.0)
         nc.vector.memset(adj_sb[:, :, NODES : NODES + 1], 1.0)
         make_identity(nc, identity[:])
+        for v, vector in enumerate((b1, ln_gamma, ln_beta)):
+            nc.scalar.dma_start(out=vector_rows[0:1, v, 0:FEAT], in_=vector.unsqueeze(0))
         nc.scalar.activation(out=table_out[:], in_=table_in[:], func=ACT.Gelu)
 
-        for v, vector in enumerate((b1, ln_gamma, ln_beta)):
-            nc.gpsimd.dma_start(out=vector_rows[0:1, v, 0:FEAT], in_=vector.unsqueeze(0))
         for q in range(2):
             nc.sync.dma_start(out=x_sb[:, 2 * q : 2 * q + 2, :], in_=x_view[:, q, :, :])
         nc.sync.dma_start(
@@ -269,32 +267,42 @@ def tile_gcnlayer_pa_kernel(tc, x, adj, W1_words, W1_scales, b1, ln_gamma, ln_be
         for q in range(CHUNKS):
             nc.sync.dma_start(out=adj_sb[:, 2 * q : 2 * q + 2, 0:NODES], in_=adj_view[:, q, :, :])
 
-        spread(0, b1_all)
+        b1_ps = acc.tile([P, BANK], F32, tag="acc")
+        spread(0, b1_ps[:])
+        nc.vector.tensor_copy(out=b1_all[:], in_=b1_ps[:, 0:FEAT])
         for q in range(CHUNKS):
             turn_x(q)
+        spread(1, gamma_beta[:, 0, :])
+        spread(2, gamma_beta[:, 1, :])
         for half in range(2):
             quantise_x(2 * half)
             quantise_x(2 * half + 1)
             for b in range(4 * half, 4 * half + 4):
                 first_product(b)
-        spread(1, gamma_all)
-        spread(2, beta_all)
 
-        for q in range(CHUNKS):
-            degrees(q)
-            turn_adj(2 * q)
-            turn_adj(2 * q + 1)
-            quantise_adj(2 * q)
-            quantise_adj(2 * q + 1)
-            if q % 2 == 1:
-                make_hs(q // 2)
+        degrees(0)
+        degrees(1)
+        degrees(2)
+        make_hs(0)
+        degrees(3)
+        turn_adj(0)
+        turn_adj(1)
+        quantise_adj(0)
+        quantise_adj(1)
+        make_hs(1)
+        for b in range(2, BLOCKS):
+            turn_adj(b)
 
-        for s in range(BLOCKS + 3):
+        for s in range(BLOCKS + 4):
             if s < BLOCKS:
                 second_product(s)
                 gelu_and_mean(s)
-            if 3 <= s:
-                finish(s - 3)
+            if 4 <= s:
+                finish(s - 4)
             if 1 <= s <= BLOCKS:
-                variance(s - 1)
+                sum_of_squares(s - 1)
                 centre_and_gain(s - 1)
+                if s % 2 == 0:
+                    inverse_std(s // 2 - 1)
+            if s + 2 < BLOCKS:
+                quantise_adj(s + 2)

@@ -252,8 +252,15 @@ def tile_gcnlayer_pa_kernel(tc, x, adj, W1_words, W1_scales, b1, ln_gamma, ln_be
             nc.scalar.dma_start(out=vector_rows[0:1, v, 0:FEAT], in_=vector.unsqueeze(0))
         nc.scalar.activation(out=table_out[:], in_=table_in[:], func=ACT.Gelu)
 
-        for q in range(2):
+        def load_x(q):
             nc.sync.dma_start(out=x_sb[:, 2 * q : 2 * q + 2, :], in_=x_view[:, q, :, :])
+
+        def load_adj(q):
+            nc.sync.dma_start(out=adj_sb[:, 2 * q : 2 * q + 2, 0:NODES], in_=adj_view[:, q, :, :])
+
+        load_x(0)
+        load_adj(1)
+        load_x(1)
         nc.sync.dma_start(
             out=w_codes[:].bitcast(I32), in_=W1_words.rearrange("g p n t -> (g p) (n t)").bitcast(I32)
         )
@@ -262,29 +269,31 @@ def tile_gcnlayer_pa_kernel(tc, x, adj, W1_words, W1_scales, b1, ln_gamma, ln_be
                 out=w_scales[32 * quadrant : 32 * quadrant + 4, :].bitcast(I32),
                 in_=W1_scales[0, 4 * quadrant : 4 * quadrant + 4, :].bitcast(I32),
             )
-        for q in range(2, CHUNKS):
-            nc.sync.dma_start(out=x_sb[:, 2 * q : 2 * q + 2, :], in_=x_view[:, q, :, :])
-        for q in range(CHUNKS):
-            nc.sync.dma_start(out=adj_sb[:, 2 * q : 2 * q + 2, 0:NODES], in_=adj_view[:, q, :, :])
+        load_x(2)
+        load_x(3)
+        load_adj(0)
+        load_adj(2)
+        load_adj(3)
 
-        b1_ps = acc.tile([P, BANK], F32, tag="acc")
-        spread(0, b1_ps[:])
-        nc.vector.tensor_copy(out=b1_all[:], in_=b1_ps[:, 0:FEAT])
-        for q in range(CHUNKS):
-            turn_x(q)
-        spread(1, gamma_beta[:, 0, :])
-        spread(2, gamma_beta[:, 1, :])
+        degrees(1)
         for half in range(2):
+            turn_x(2 * half)
+            turn_x(2 * half + 1)
+            if half == 0:
+                b1_ps = acc.tile([P, BANK], F32, tag="acc")
+                spread(0, b1_ps[:])
+                nc.vector.tensor_copy(out=b1_all[:], in_=b1_ps[:, 0:FEAT])
             quantise_x(2 * half)
             quantise_x(2 * half + 1)
             for b in range(4 * half, 4 * half + 4):
                 first_product(b)
+        spread(1, gamma_beta[:, 0, :])
+        spread(2, gamma_beta[:, 1, :])
 
         degrees(0)
-        degrees(1)
         degrees(2)
-        make_hs(0)
         degrees(3)
+        make_hs(0)
         turn_adj(0)
         turn_adj(1)
         quantise_adj(0)

@@ -48,6 +48,7 @@ def tile_gcnlayer_pa_kernel(tc, x, adj, W1_words, W1_scales, b1, ln_gamma, ln_be
         adj_grouped = keep.tile([P, BLOCKS, PASSES, P, PACK], BF16, align_bytes=64)
         adj_codes = keep.tile([P, BLOCKS, PASSES, P], U32, align_bytes=64)
         adj_scales = keep.tile([P, BLOCKS, PASSES, P], U8, align_bytes=64)
+        hs_rows = keep.tile([P, BLOCKS, FEAT], BF16)
         hs_grouped = keep.tile([P, PASSES, FEAT, PACK], BF16, align_bytes=64)
         hs_codes = keep.tile([P, PASSES, FEAT], U32, align_bytes=64)
         hs_scales = keep.tile([P, PASSES, FEAT], U8, align_bytes=64)
@@ -158,14 +159,16 @@ def tile_gcnlayer_pa_kernel(tc, x, adj, W1_words, W1_scales, b1, ln_gamma, ln_be
                 in_=adj_grouped[:, b, :, :, :].rearrange("p c i t -> p (c i t)"),
             )
 
-        def make_hs(c):
-            four = slice(4 * c, 4 * c + 4)
-            nc.vector.tensor_tensor(
-                out=hs_grouped[:, c, :, :],
-                in0=h_bias[:, four, :].rearrange("p t f -> p f t"),
-                in1=dinv[:, four].unsqueeze(1).to_broadcast([P, FEAT, PACK]),
-                op=ALU.mult,
+        def scale_hs(b):
+            nc.vector.tensor_scalar_mul(out=hs_rows[:, b, :], in0=h_bias[:, b, :], scalar1=dinv[:, b : b + 1])
+
+        def group_hs(c):
+            nc.vector.tensor_copy(
+                out=hs_grouped[:, c, :, :].rearrange("p (r i) t -> p r t i", i=4),
+                in_=hs_rows[:, 4 * c : 4 * c + 4, :].rearrange("p t (r i) -> p r t i", i=4),
             )
+
+        def quantise_hs(c):
             for f0, width in FEAT_CUTS:
                 nc.vector.quantize_mx(
                     out=hs_codes[:, c, f0 : f0 + width].bitcast(FP8X4),
@@ -293,12 +296,20 @@ def tile_gcnlayer_pa_kernel(tc, x, adj, W1_words, W1_scales, b1, ln_gamma, ln_be
         degrees(0)
         degrees(2)
         degrees(3)
-        make_hs(0)
         turn_adj(0)
         turn_adj(1)
+        for b in range(4):
+            scale_hs(b)
+        scale_hs(4)
+        group_hs(0)
+        scale_hs(5)
+        quantise_hs(0)
+        scale_hs(6)
+        scale_hs(7)
         quantise_adj(0)
+        group_hs(1)
         quantise_adj(1)
-        make_hs(1)
+        quantise_hs(1)
         for b in range(2, BLOCKS):
             turn_adj(b)
 

@@ -23,6 +23,7 @@ BANK = 512
 FEAT_CUTS = ((0, 256), (256, 128))
 SELF_LOOP = 16
 ROW = NODES + SELF_LOOP
+FINISH_LAG = 6
 
 FLOPS = 2 * NODES * K_IN * FEAT + 2 * NODES * NODES * FEAT
 
@@ -118,26 +119,34 @@ def tile_gcnlayer_pa_kernel(tc, x, adj, W1_words, W1_scales, b1, ln_gamma, ln_be
                 )
             nc.vector.tensor_tensor(out=h_bias[:, b, :], in0=h_ps[:], in1=b1_all[:], op=ALU.add)
 
-        def degrees(q):
+        def row_sum(b):
+            c, t = divmod(b, PACK)
+            u, e = divmod(t, 2)
+            row = adj_sb[:, b, :]
+            if u == 0:
+                nc.scalar.activation(
+                    out=row_copy[:, c, e, :], in_=row, func=ACT.Copy, accum_out=deg_scalar[:, c, e : e + 1]
+                )
+            else:
+                nc.vector.scalar_tensor_tensor(
+                    out=pair_sums[:, c, e, :],
+                    in0=row[:, 0 : ROW // 2],
+                    scalar=1.0,
+                    in1=row[:, ROW // 2 : ROW],
+                    op0=ALU.mult,
+                    op1=ALU.add,
+                    accum_out=deg_vector[:, c, e : e + 1],
+                )
+
+        def inverse_sqrt_degree(q):
             c, u = divmod(q, 2)
-            for e in range(2):
-                row = adj_sb[:, 2 * q + e, :]
-                if u == 0:
-                    nc.scalar.activation(
-                        out=row_copy[:, c, e, :], in_=row, func=ACT.Copy, accum_out=deg_scalar[:, c, e : e + 1]
-                    )
-                else:
-                    nc.vector.scalar_tensor_tensor(
-                        out=pair_sums[:, c, e, :],
-                        in0=row[:, 0 : ROW // 2],
-                        scalar=1.0,
-                        in1=row[:, ROW // 2 : ROW],
-                        op0=ALU.mult,
-                        op1=ALU.add,
-                        accum_out=deg_vector[:, c, e : e + 1],
-                    )
             deg = deg_scalar if u == 0 else deg_vector
             nc.gpsimd.tensor_tensor(out=dinv[:, 2 * q : 2 * q + 2], in0=deg[:, c, :], in1=minus_half[:], op=ALU.pow)
+
+        def degrees(q):
+            row_sum(2 * q)
+            row_sum(2 * q + 1)
+            inverse_sqrt_degree(q)
 
         def turn_adj(b):
             adj_words = adj_sb[:, b, 0:NODES].bitcast(F32)
@@ -160,7 +169,10 @@ def tile_gcnlayer_pa_kernel(tc, x, adj, W1_words, W1_scales, b1, ln_gamma, ln_be
             )
 
         def scale_hs(b):
-            nc.vector.tensor_scalar_mul(out=hs_rows[:, b, :], in0=h_bias[:, b, :], scalar1=dinv[:, b : b + 1])
+            if b < BLOCKS // PASSES:
+                nc.scalar.activation(out=hs_rows[:, b, :], in_=h_bias[:, b, :], func=ACT.Copy, scale=dinv[:, b : b + 1])
+            else:
+                nc.vector.tensor_scalar_mul(out=hs_rows[:, b, :], in0=h_bias[:, b, :], scalar1=dinv[:, b : b + 1])
 
         def group_hs(c):
             nc.vector.tensor_copy(
@@ -262,7 +274,7 @@ def tile_gcnlayer_pa_kernel(tc, x, adj, W1_words, W1_scales, b1, ln_gamma, ln_be
             nc.sync.dma_start(out=adj_sb[:, 2 * q : 2 * q + 2, 0:NODES], in_=adj_view[:, q, :, :])
 
         load_x(0)
-        load_adj(1)
+        load_adj(0)
         load_x(1)
         nc.sync.dma_start(
             out=w_codes[:].bitcast(I32), in_=W1_words.rearrange("g p n t -> (g p) (n t)").bitcast(I32)
@@ -272,40 +284,46 @@ def tile_gcnlayer_pa_kernel(tc, x, adj, W1_words, W1_scales, b1, ln_gamma, ln_be
                 out=w_scales[32 * quadrant : 32 * quadrant + 4, :].bitcast(I32),
                 in_=W1_scales[0, 4 * quadrant : 4 * quadrant + 4, :].bitcast(I32),
             )
+        load_adj(1)
         load_x(2)
         load_x(3)
-        load_adj(0)
         load_adj(2)
         load_adj(3)
 
+        turn_x(0)
+        row_sum(0)
+        b1_ps = acc.tile([P, BANK], F32, tag="acc")
+        spread(0, b1_ps[:])
+        nc.vector.tensor_copy(out=b1_all[:], in_=b1_ps[:, 0:FEAT])
+        quantise_x(0)
+        turn_x(1)
+        row_sum(1)
+        inverse_sqrt_degree(0)
+        quantise_x(1)
+        for b in range(4):
+            first_product(b)
         degrees(1)
-        for half in range(2):
-            turn_x(2 * half)
-            turn_x(2 * half + 1)
-            if half == 0:
-                b1_ps = acc.tile([P, BANK], F32, tag="acc")
-                spread(0, b1_ps[:])
-                nc.vector.tensor_copy(out=b1_all[:], in_=b1_ps[:, 0:FEAT])
-            quantise_x(2 * half)
-            quantise_x(2 * half + 1)
-            for b in range(4 * half, 4 * half + 4):
-                first_product(b)
+        turn_x(2)
+        turn_x(3)
+        quantise_x(2)
+        quantise_x(3)
+        for b in range(4, BLOCKS):
+            first_product(b)
         spread(1, gamma_beta[:, 0, :])
         spread(2, gamma_beta[:, 1, :])
-
-        degrees(0)
         degrees(2)
         degrees(3)
-        turn_adj(0)
-        turn_adj(1)
+
         for b in range(4):
             scale_hs(b)
+        turn_adj(0)
+        turn_adj(1)
         scale_hs(4)
-        group_hs(0)
         scale_hs(5)
-        quantise_hs(0)
+        group_hs(0)
         scale_hs(6)
         scale_hs(7)
+        quantise_hs(0)
         quantise_adj(0)
         group_hs(1)
         quantise_adj(1)
@@ -313,12 +331,12 @@ def tile_gcnlayer_pa_kernel(tc, x, adj, W1_words, W1_scales, b1, ln_gamma, ln_be
         for b in range(2, BLOCKS):
             turn_adj(b)
 
-        for s in range(BLOCKS + 4):
+        for s in range(BLOCKS + FINISH_LAG):
             if s < BLOCKS:
                 second_product(s)
                 gelu_and_mean(s)
-            if 4 <= s:
-                finish(s - 4)
+            if FINISH_LAG <= s:
+                finish(s - FINISH_LAG)
             if 1 <= s <= BLOCKS:
                 sum_of_squares(s - 1)
                 centre_and_gain(s - 1)

@@ -16,14 +16,16 @@ NODES = 1024
 K_IN = 512
 FEAT = 384
 EPS = 1e-6
+SELF_LOOP = 16
+ROW = NODES + SELF_LOOP
 BLOCKS = NODES // P
 PASSES = NODES // (P * PACK)
 CHUNKS = BLOCKS // 2
 BANK = 512
 FEAT_CUTS = ((0, 256), (256, 128))
-SELF_LOOP = 16
-ROW = NODES + SELF_LOOP
 FINISH_LAG = 6
+TENSOR_CHUNKS = (1, 2)
+ORDER = (2, 3, 0, 1, 4, 5, 6, 7)
 
 FLOPS = 2 * NODES * K_IN * FEAT + 2 * NODES * NODES * FEAT
 
@@ -56,17 +58,18 @@ def tile_gcnlayer_pa_kernel(tc, x, adj, W1_words, W1_scales, b1, ln_gamma, ln_be
 
         identity = keep.tile([P, P], F32)
         ones = keep.tile([P, P], BF16)
-        vector_rows = keep.tile([P, 3, BANK], BF16)
+        vector_rows = keep.tile([P, 3, FEAT], BF16)
         b1_all = keep.tile([P, FEAT], F32)
-        gamma_beta = fixed.tile([P, 2, BANK], BF16)
-        minus_half = keep.tile([P, 2], F32)
+        shared_bank = fixed.tile([P, BANK], F32)
+        gamma_beta = shared_bank[:, 0:FEAT].bitcast(BF16).rearrange("p (v f) -> p v f", v=2)
+        deg_ps = shared_bank[:, FEAT : FEAT + BLOCKS]
+        minus_half = keep.tile([P, 4], F32)
         table_in = keep.tile([P, 1], F32)
         table_out = keep.tile([P, 1], F32)
 
-        pair_sums = keep.tile([P, PASSES, 2, ROW // 2], F32)
-        row_copy = keep.tile([P, PASSES, 2, ROW], BF16)
-        deg_scalar = keep.tile([P, PASSES, 2], F32)
-        deg_vector = keep.tile([P, PASSES, 2], F32)
+        row_copy = keep.tile([P, BLOCKS, ROW], BF16)
+        pair_sums = keep.tile([P, 2, ROW // 2], F32)
+        deg = keep.tile([P, BLOCKS, 8], F32)
         dinv = keep.tile([P, BLOCKS], F32)
 
         h_bias = keep.tile([P, BLOCKS, FEAT], F32)
@@ -120,37 +123,42 @@ def tile_gcnlayer_pa_kernel(tc, x, adj, W1_words, W1_scales, b1, ln_gamma, ln_be
             nc.vector.tensor_tensor(out=h_bias[:, b, :], in0=h_ps[:], in1=b1_all[:], op=ALU.add)
 
         def row_sum(b):
-            c, t = divmod(b, PACK)
-            u, e = divmod(t, 2)
-            row = adj_sb[:, b, :]
-            if u == 0:
-                nc.scalar.activation(
-                    out=row_copy[:, c, e, :], in_=row, func=ACT.Copy, accum_out=deg_scalar[:, c, e : e + 1]
-                )
-            else:
-                nc.vector.scalar_tensor_tensor(
-                    out=pair_sums[:, c, e, :],
-                    in0=row[:, 0 : ROW // 2],
-                    scalar=1.0,
-                    in1=row[:, ROW // 2 : ROW],
-                    op0=ALU.mult,
-                    op1=ALU.add,
-                    accum_out=deg_vector[:, c, e : e + 1],
-                )
-
-        def inverse_sqrt_degree(q):
-            c, u = divmod(q, 2)
-            deg = deg_scalar if u == 0 else deg_vector
-            nc.gpsimd.tensor_tensor(out=dinv[:, 2 * q : 2 * q + 2], in0=deg[:, c, :], in1=minus_half[:], op=ALU.pow)
+            for c in range(PASSES):
+                for t in range(PACK):
+                    nc.tensor.matmul(
+                        out=deg_ps[:, b : b + 1],
+                        lhsT=adj_grouped[:, b, c, :, t],
+                        rhs=ones[:, 0:1],
+                        start=(c == 0 and t == 0),
+                        stop=(c == PASSES - 1 and t == PACK - 1),
+                    )
 
         def degrees(q):
-            row_sum(2 * q)
-            row_sum(2 * q + 1)
-            inverse_sqrt_degree(q)
+            both = slice(2 * q, 2 * q + 2)
+            nc.gpsimd.tensor_tensor(out=dinv[:, both], in0=deg[:, both, 0], in1=minus_half[:, 0:2], op=ALU.pow)
 
-        def turn_adj(b):
+        def tensor_degrees():
+            nc.scalar.add(out=deg[:, 2:4, 0], in_=deg_ps[:, 2:4], add=1.0)
+            nc.gpsimd.tensor_tensor(out=dinv[:, 2:4], in0=deg[:, 2:4, 0], in1=minus_half[:, 0:2], op=ALU.pow)
+
+        def row_sum_scalar(b):
+            nc.scalar.activation(out=row_copy[:, b, :], in_=adj_sb[:, b, :], func=ACT.Copy, accum_out=deg[:, b, 0:1])
+
+        def row_sum_vector(b):
+            row = adj_sb[:, b, :]
+            nc.vector.scalar_tensor_tensor(
+                out=pair_sums[:, b % 2, :],
+                in0=row[:, 0 : ROW // 2],
+                scalar=1.0,
+                in1=row[:, ROW // 2 : ROW],
+                op0=ALU.mult,
+                op1=ALU.add,
+                accum_out=deg[:, b, 0:1],
+            )
+
+        def turn_adj(b, pool=turn, tag="turn"):
             adj_words = adj_sb[:, b, 0:NODES].bitcast(F32)
-            adj_turned = turn.tile([P, PASSES, 2, P], F32, tag="turn")
+            adj_turned = pool.tile([P, PASSES, 2, P], F32, tag=tag)
             for c in range(PASSES):
                 for u in range(2):
                     first = (2 * c + u) * P
@@ -169,7 +177,7 @@ def tile_gcnlayer_pa_kernel(tc, x, adj, W1_words, W1_scales, b1, ln_gamma, ln_be
             )
 
         def scale_hs(b):
-            if b < BLOCKS // PASSES:
+            if b not in (2, 3):
                 nc.scalar.activation(out=hs_rows[:, b, :], in_=h_bias[:, b, :], func=ACT.Copy, scale=dinv[:, b : b + 1])
             else:
                 nc.vector.tensor_scalar_mul(out=hs_rows[:, b, :], in0=h_bias[:, b, :], scalar1=dinv[:, b : b + 1])
@@ -201,6 +209,9 @@ def tile_gcnlayer_pa_kernel(tc, x, adj, W1_words, W1_scales, b1, ln_gamma, ln_be
                         start=(c == 0),
                         stop=(c == PASSES - 1),
                     )
+            return agg_ps
+
+        def add_hs(b, agg_ps):
             nc.vector.scalar_tensor_tensor(
                 out=pre[:, b, :],
                 in0=h_bias[:, b, :],
@@ -215,7 +226,9 @@ def tile_gcnlayer_pa_kernel(tc, x, adj, W1_words, W1_scales, b1, ln_gamma, ln_be
             nc.scalar.activation(
                 out=g[:, b, :], in_=pre[:, b, :], func=ACT.Gelu, scale=dinv[:, one], accum_out=g_sum[:, one]
             )
-            nc.scalar.mul(out=minus_mean[:, one], in_=g_sum[:, one], mul=-1.0 / FEAT)
+            nc.gpsimd.tensor_scalar(
+                out=minus_mean[:, one], in0=g_sum[:, one], scalar1=-1.0 / FEAT, scalar2=0.0, op0=ALU.mult, op1=ALU.add
+            )
 
         def sum_of_squares(b):
             one = slice(b, b + 1)
@@ -223,23 +236,24 @@ def tile_gcnlayer_pa_kernel(tc, x, adj, W1_words, W1_scales, b1, ln_gamma, ln_be
                 out=squares[:, b, :],
                 in_=g[:, b, :],
                 func=ACT.Square,
-                bias=minus_mean[:, one],
+                scale=-1.0 * FEAT,
+                bias=g_sum[:, one],
                 accum_out=square_sum[:, one],
             )
 
         def inverse_std(q):
             both = slice(2 * q, 2 * q + 2)
             nc.gpsimd.tensor_scalar(
-                out=var_eps[:, both], in0=square_sum[:, both], scalar1=1.0 / FEAT, scalar2=EPS, op0=ALU.mult, op1=ALU.add
+                out=var_eps[:, both], in0=square_sum[:, both], scalar1=1.0 / FEAT**3, scalar2=EPS, op0=ALU.mult, op1=ALU.add
             )
-            nc.gpsimd.tensor_tensor(out=rstd[:, both], in0=var_eps[:, both], in1=minus_half[:], op=ALU.pow)
+            nc.gpsimd.tensor_tensor(out=rstd[:, both], in0=var_eps[:, both], in1=minus_half[:, 0:2], op=ALU.pow)
 
         def centre_and_gain(b):
             nc.vector.scalar_tensor_tensor(
                 out=scaled[:, b, :],
                 in0=g[:, b, :],
                 scalar=minus_mean[:, b : b + 1],
-                in1=gamma_beta[:, 0, 0:FEAT],
+                in1=gamma_beta[:, 0, :],
                 op0=ALU.add,
                 op1=ALU.mult,
             )
@@ -249,22 +263,21 @@ def tile_gcnlayer_pa_kernel(tc, x, adj, W1_words, W1_scales, b1, ln_gamma, ln_be
                 out=result[:, b, :],
                 in0=scaled[:, b, :],
                 scalar=rstd[:, b : b + 1],
-                in1=gamma_beta[:, 1, 0:FEAT],
+                in1=gamma_beta[:, 1, :],
                 op0=ALU.mult,
                 op1=ALU.add,
             )
             nc.sync.dma_start(out=out_view[:, b // 2, b % 2, :], in_=result[:, b, :])
 
+        nc.vector.memset(table_in[:], 0.0)
         nc.vector.memset(w_scales[:].bitcast(I32), 0)
-        nc.vector.memset(vector_rows[:], 0.0)
+        for v in range(3):
+            nc.vector.memset(vector_rows[:, v, :].bitcast(U32), 0)
         nc.vector.memset(ones[:], 1.0)
         nc.vector.memset(minus_half[:], -0.5)
-        nc.vector.memset(table_in[:], 0.0)
         nc.vector.memset(adj_sb[:, :, NODES:ROW], 0.0)
         nc.vector.memset(adj_sb[:, :, NODES : NODES + 1], 1.0)
         make_identity(nc, identity[:])
-        for v, vector in enumerate((b1, ln_gamma, ln_beta)):
-            nc.scalar.dma_start(out=vector_rows[0:1, v, 0:FEAT], in_=vector.unsqueeze(0))
         nc.scalar.activation(out=table_out[:], in_=table_in[:], func=ACT.Gelu)
 
         def load_x(q):
@@ -274,7 +287,6 @@ def tile_gcnlayer_pa_kernel(tc, x, adj, W1_words, W1_scales, b1, ln_gamma, ln_be
             nc.sync.dma_start(out=adj_sb[:, 2 * q : 2 * q + 2, 0:NODES], in_=adj_view[:, q, :, :])
 
         load_x(0)
-        load_adj(0)
         load_x(1)
         nc.sync.dma_start(
             out=w_codes[:].bitcast(I32), in_=W1_words.rearrange("g p n t -> (g p) (n t)").bitcast(I32)
@@ -284,63 +296,83 @@ def tile_gcnlayer_pa_kernel(tc, x, adj, W1_words, W1_scales, b1, ln_gamma, ln_be
                 out=w_scales[32 * quadrant : 32 * quadrant + 4, :].bitcast(I32),
                 in_=W1_scales[0, 4 * quadrant : 4 * quadrant + 4, :].bitcast(I32),
             )
-        load_adj(1)
+        for v, vector in enumerate((b1, ln_gamma, ln_beta)):
+            nc.gpsimd.dma_start(out=vector_rows[0:1, v, :], in_=vector.unsqueeze(0))
         load_x(2)
         load_x(3)
-        load_adj(2)
-        load_adj(3)
+        for q in range(CHUNKS):
+            load_adj(q)
 
         turn_x(0)
-        row_sum(0)
-        b1_ps = acc.tile([P, BANK], F32, tag="acc")
-        spread(0, b1_ps[:])
-        nc.vector.tensor_copy(out=b1_all[:], in_=b1_ps[:, 0:FEAT])
-        quantise_x(0)
         turn_x(1)
-        row_sum(1)
-        inverse_sqrt_degree(0)
-        quantise_x(1)
-        for b in range(4):
-            first_product(b)
-        degrees(1)
+        b1_ps = acc.tile([P, BANK], F32, tag="acc")
+        spread(0, b1_ps[:, 0:FEAT])
+        quantise_x(0)
+        nc.vector.tensor_copy(out=b1_all[:], in_=b1_ps[:, 0:FEAT])
         turn_x(2)
-        turn_x(3)
+        quantise_x(1)
+        first_product(0)
+        first_product(1)
         quantise_x(2)
+        turn_x(3)
+        first_product(2)
+        first_product(3)
         quantise_x(3)
-        for b in range(4, BLOCKS):
-            first_product(b)
-        spread(1, gamma_beta[:, 0, :])
-        spread(2, gamma_beta[:, 1, :])
+        row_sum_scalar(0)
+        turn_adj(2)
+        first_product(4)
+        first_product(5)
+        row_sum_scalar(1)
+        degrees(0)
+        turn_adj(3)
+        first_product(6)
+        first_product(7)
+        row_sum(2)
+        row_sum(3)
+        row_sum_scalar(5)
+        tensor_degrees()
+        row_sum_vector(4)
         degrees(2)
+        row_sum_vector(6)
+        row_sum_vector(7)
         degrees(3)
-
-        for b in range(4):
-            scale_hs(b)
-        turn_adj(0)
-        turn_adj(1)
+        quantise_adj(2)
+        scale_hs(2)
+        scale_hs(3)
+        scale_hs(0)
+        scale_hs(1)
         scale_hs(4)
         scale_hs(5)
-        group_hs(0)
         scale_hs(6)
         scale_hs(7)
-        quantise_hs(0)
-        quantise_adj(0)
+        quantise_adj(3)
+        group_hs(0)
+        turn_adj(0)
+        turn_adj(1)
+        turn_adj(4)
+        turn_adj(5, acc, "acc")
+        turn_adj(6, acc, "acc")
+        turn_adj(7, acc, "acc")
         group_hs(1)
-        quantise_adj(1)
+        quantise_hs(0)
+        spread(1, gamma_beta[:, 0, :])
+        spread(2, gamma_beta[:, 1, :])
         quantise_hs(1)
-        for b in range(2, BLOCKS):
-            turn_adj(b)
+        quantise_adj(0)
 
+        products = {0: second_product(ORDER[0])}
         for s in range(BLOCKS + FINISH_LAG):
+            if s + 1 < BLOCKS:
+                products[s + 1] = second_product(ORDER[s + 1])
             if s < BLOCKS:
-                second_product(s)
-                gelu_and_mean(s)
+                add_hs(ORDER[s], products[s])
+                gelu_and_mean(ORDER[s])
             if FINISH_LAG <= s:
-                finish(s - FINISH_LAG)
+                finish(ORDER[s - FINISH_LAG])
+            if s + 3 < BLOCKS:
+                quantise_adj(ORDER[s + 3])
             if 1 <= s <= BLOCKS:
-                sum_of_squares(s - 1)
-                centre_and_gain(s - 1)
-                if s % 2 == 0:
-                    inverse_std(s // 2 - 1)
-            if s + 2 < BLOCKS:
-                quantise_adj(s + 2)
+                sum_of_squares(ORDER[s - 1])
+                centre_and_gain(ORDER[s - 1])
+            if s % 2 == 1 and 3 <= s < BLOCKS or s == BLOCKS:
+                inverse_std(ORDER[(s - 2) // 2 * 2] // 2)

@@ -60,6 +60,7 @@ def tile_gcnlayer_pa_kernel(tc, x, adj, W1_words, W1_scales, b1, ln_gamma, ln_be
         ones = keep.tile([P, P], BF16)
         vector_rows = keep.tile([P, 3, FEAT], BF16)
         b1_all = keep.tile([P, FEAT], F32)
+        beta_all = keep.tile([P, FEAT], F32)
         shared_bank = fixed.tile([P, BANK], F32)
         gamma_beta = shared_bank[:, 0:FEAT].bitcast(BF16).rearrange("p (v f) -> p v f", v=2)
         deg_ps = shared_bank[:, FEAT : FEAT + BLOCKS]
@@ -134,12 +135,12 @@ def tile_gcnlayer_pa_kernel(tc, x, adj, W1_words, W1_scales, b1, ln_gamma, ln_be
                     )
 
         def degrees(q):
-            both = slice(2 * q, 2 * q + 2)
-            nc.gpsimd.tensor_tensor(out=dinv[:, both], in0=deg[:, both, 0], in1=minus_half[:, 0:2], op=ALU.pow)
+            both = slice(4 * q, 4 * q + 4)
+            nc.gpsimd.tensor_tensor(out=dinv[:, both], in0=deg[:, both, 0], in1=minus_half[:], op=ALU.pow)
 
         def tensor_degrees():
             nc.scalar.add(out=deg[:, 2:4, 0], in_=deg_ps[:, 2:4], add=1.0)
-            nc.gpsimd.tensor_tensor(out=dinv[:, 2:4], in0=deg[:, 2:4, 0], in1=minus_half[:, 0:2], op=ALU.pow)
+            degrees(0)
 
         def row_sum_scalar(b):
             nc.scalar.activation(out=row_copy[:, b, :], in_=adj_sb[:, b, :], func=ACT.Copy, accum_out=deg[:, b, 0:1])
@@ -177,7 +178,7 @@ def tile_gcnlayer_pa_kernel(tc, x, adj, W1_words, W1_scales, b1, ln_gamma, ln_be
             )
 
         def scale_hs(b):
-            if b not in (2, 3):
+            if b not in (2, 3, 6, 7):
                 nc.scalar.activation(out=hs_rows[:, b, :], in_=h_bias[:, b, :], func=ACT.Copy, scale=dinv[:, b : b + 1])
             else:
                 nc.vector.tensor_scalar_mul(out=hs_rows[:, b, :], in0=h_bias[:, b, :], scalar1=dinv[:, b : b + 1])
@@ -226,9 +227,10 @@ def tile_gcnlayer_pa_kernel(tc, x, adj, W1_words, W1_scales, b1, ln_gamma, ln_be
             nc.scalar.activation(
                 out=g[:, b, :], in_=pre[:, b, :], func=ACT.Gelu, scale=dinv[:, one], accum_out=g_sum[:, one]
             )
-            nc.gpsimd.tensor_scalar(
-                out=minus_mean[:, one], in0=g_sum[:, one], scalar1=-1.0 / FEAT, scalar2=0.0, op0=ALU.mult, op1=ALU.add
-            )
+
+        def mean(b):
+            one = slice(b, b + 1)
+            nc.gpsimd.tensor_scalar(out=minus_mean[:, one], in0=g_sum[:, one], scalar1=-1.0 / FEAT, scalar2=0.0, op0=ALU.mult, op1=ALU.add)
 
         def sum_of_squares(b):
             one = slice(b, b + 1)
@@ -241,12 +243,12 @@ def tile_gcnlayer_pa_kernel(tc, x, adj, W1_words, W1_scales, b1, ln_gamma, ln_be
                 accum_out=square_sum[:, one],
             )
 
-        def inverse_std(q):
-            both = slice(2 * q, 2 * q + 2)
+        def inverse_std(b, count):
+            both = slice(b, b + count)
             nc.gpsimd.tensor_scalar(
                 out=var_eps[:, both], in0=square_sum[:, both], scalar1=1.0 / FEAT**3, scalar2=EPS, op0=ALU.mult, op1=ALU.add
             )
-            nc.gpsimd.tensor_tensor(out=rstd[:, both], in0=var_eps[:, both], in1=minus_half[:, 0:2], op=ALU.pow)
+            nc.gpsimd.tensor_tensor(out=rstd[:, both], in0=var_eps[:, both], in1=minus_half[:, 0:count], op=ALU.pow)
 
         def centre_and_gain(b):
             nc.vector.scalar_tensor_tensor(
@@ -257,6 +259,13 @@ def tile_gcnlayer_pa_kernel(tc, x, adj, W1_words, W1_scales, b1, ln_gamma, ln_be
                 op0=ALU.add,
                 op1=ALU.mult,
             )
+
+        def finish_gpsimd(b):
+            nc.gpsimd.tensor_scalar(
+                out=scaled[:, b, :], in0=scaled[:, b, :], scalar1=rstd[:, b : b + 1], scalar2=0.0, op0=ALU.mult, op1=ALU.add
+            )
+            nc.gpsimd.tensor_tensor(out=result[:, b, :], in0=scaled[:, b, :], in1=beta_all[:], op=ALU.add)
+            nc.sync.dma_start(out=out_view[:, b // 2, b % 2, :], in_=result[:, b, :])
 
         def finish(b):
             nc.vector.scalar_tensor_tensor(
@@ -307,58 +316,56 @@ def tile_gcnlayer_pa_kernel(tc, x, adj, W1_words, W1_scales, b1, ln_gamma, ln_be
         turn_x(1)
         b1_ps = acc.tile([P, BANK], F32, tag="acc")
         spread(0, b1_ps[:, 0:FEAT])
+        turn_x(2)
+        turn_x(3)
         quantise_x(0)
         nc.vector.tensor_copy(out=b1_all[:], in_=b1_ps[:, 0:FEAT])
-        turn_x(2)
         quantise_x(1)
         first_product(0)
         first_product(1)
         quantise_x(2)
-        turn_x(3)
         first_product(2)
-        first_product(3)
         quantise_x(3)
+        first_product(3)
         row_sum_scalar(0)
         turn_adj(2)
+        turn_adj(3)
         first_product(4)
         first_product(5)
         row_sum_scalar(1)
-        degrees(0)
-        turn_adj(3)
         first_product(6)
         first_product(7)
         row_sum(2)
         row_sum(3)
-        row_sum_scalar(5)
         tensor_degrees()
         row_sum_vector(4)
-        degrees(2)
+        row_sum_scalar(5)
         row_sum_vector(6)
         row_sum_vector(7)
-        degrees(3)
+        degrees(1)
         quantise_adj(2)
         scale_hs(2)
         scale_hs(3)
         scale_hs(0)
         scale_hs(1)
+        turn_adj(0)
         scale_hs(4)
         scale_hs(5)
-        scale_hs(6)
-        scale_hs(7)
         quantise_adj(3)
-        group_hs(0)
-        turn_adj(0)
         turn_adj(1)
         turn_adj(4)
+        group_hs(0)
+        scale_hs(6)
+        scale_hs(7)
         turn_adj(5, acc, "acc")
         turn_adj(6, acc, "acc")
         turn_adj(7, acc, "acc")
-        group_hs(1)
         quantise_hs(0)
+        group_hs(1)
         spread(1, gamma_beta[:, 0, :])
         spread(2, gamma_beta[:, 1, :])
-        quantise_hs(1)
         quantise_adj(0)
+        quantise_hs(1)
 
         products = {0: second_product(ORDER[0])}
         for s in range(BLOCKS + FINISH_LAG):
@@ -367,12 +374,18 @@ def tile_gcnlayer_pa_kernel(tc, x, adj, W1_words, W1_scales, b1, ln_gamma, ln_be
             if s < BLOCKS:
                 add_hs(ORDER[s], products[s])
                 gelu_and_mean(ORDER[s])
-            if FINISH_LAG <= s:
-                finish(ORDER[s - FINISH_LAG])
-            if s + 3 < BLOCKS:
-                quantise_adj(ORDER[s + 3])
+                mean(ORDER[s])
             if 1 <= s <= BLOCKS:
                 sum_of_squares(ORDER[s - 1])
-                centre_and_gain(ORDER[s - 1])
-            if s % 2 == 1 and 3 <= s < BLOCKS or s == BLOCKS:
-                inverse_std(ORDER[(s - 2) // 2 * 2] // 2)
+
+            if s + 3 < BLOCKS:
+                quantise_adj(ORDER[s + 3])
+            if 2 <= s < BLOCKS + 2:
+                centre_and_gain(ORDER[s - 2])
+            if FINISH_LAG <= s:
+                if s - FINISH_LAG in ():
+                    finish_gpsimd(ORDER[s - FINISH_LAG])
+                else:
+                    finish(ORDER[s - FINISH_LAG])
+            if s in (2, 4, 6, 8):
+                inverse_std(ORDER[s - 2], 2)

@@ -51,7 +51,7 @@ def tile_gcnlayer_pa_kernel(tc, x, adj, W1_words, W1_scales, b1, ln_gamma, ln_be
         adj_grouped = keep.tile([P, BLOCKS, PASSES, P, PACK], BF16, align_bytes=64)
         adj_codes = keep.tile([P, BLOCKS, PASSES, P], U32, align_bytes=64)
         adj_scales = keep.tile([P, BLOCKS, PASSES, P], U8, align_bytes=64)
-        hs_rows = keep.tile([P, BLOCKS, FEAT], BF16)
+        hs_pairs = keep.tile([P, CHUNKS, FEAT, 2], BF16)
         hs_grouped = keep.tile([P, PASSES, FEAT, PACK], BF16, align_bytes=64)
         hs_codes = keep.tile([P, PASSES, FEAT], U32, align_bytes=64)
         hs_scales = keep.tile([P, PASSES, FEAT], U8, align_bytes=64)
@@ -60,11 +60,10 @@ def tile_gcnlayer_pa_kernel(tc, x, adj, W1_words, W1_scales, b1, ln_gamma, ln_be
         ones = keep.tile([P, P], BF16)
         vector_rows = keep.tile([P, 3, FEAT], BF16)
         b1_all = keep.tile([P, FEAT], F32)
-        beta_all = keep.tile([P, FEAT], F32)
         shared_bank = fixed.tile([P, BANK], F32)
         gamma_beta = shared_bank[:, 0:FEAT].bitcast(BF16).rearrange("p (v f) -> p v f", v=2)
         deg_ps = shared_bank[:, FEAT : FEAT + BLOCKS]
-        minus_half = keep.tile([P, 4], F32)
+        minus_half = keep.tile([P, BLOCKS], F32)
         table_in = keep.tile([P, 1], F32)
         table_out = keep.tile([P, 1], F32)
 
@@ -134,13 +133,18 @@ def tile_gcnlayer_pa_kernel(tc, x, adj, W1_words, W1_scales, b1, ln_gamma, ln_be
                         stop=(c == PASSES - 1 and t == PACK - 1),
                     )
 
-        def degrees(q):
-            both = slice(4 * q, 4 * q + 4)
-            nc.gpsimd.tensor_tensor(out=dinv[:, both], in0=deg[:, both, 0], in1=minus_half[:], op=ALU.pow)
+        def degrees(b, count):
+            some = slice(b, b + count)
+            nc.gpsimd.tensor_tensor(out=dinv[:, some], in0=deg[:, some, 0], in1=minus_half[:, 0:count], op=ALU.pow)
 
-        def tensor_degrees():
+        def tensor_degrees(b, count):
+            some = slice(b, b + count)
+            nc.scalar.add(out=deg[:, some, 0], in_=deg_ps[:, some], add=1.0)
+            degrees(b, count)
+
+        def tensor_degrees2():
             nc.scalar.add(out=deg[:, 2:4, 0], in_=deg_ps[:, 2:4], add=1.0)
-            degrees(0)
+            degrees(0, 4)
 
         def row_sum_scalar(b):
             nc.scalar.activation(out=row_copy[:, b, :], in_=adj_sb[:, b, :], func=ACT.Copy, accum_out=deg[:, b, 0:1])
@@ -178,15 +182,15 @@ def tile_gcnlayer_pa_kernel(tc, x, adj, W1_words, W1_scales, b1, ln_gamma, ln_be
             )
 
         def scale_hs(b):
-            if b not in (2, 3, 6, 7):
-                nc.scalar.activation(out=hs_rows[:, b, :], in_=h_bias[:, b, :], func=ACT.Copy, scale=dinv[:, b : b + 1])
+            if b in (0, 1, 4, 5):
+                nc.scalar.activation(out=hs_pairs[:, b // 2, :, b % 2], in_=h_bias[:, b, :], func=ACT.Copy, scale=dinv[:, b : b + 1])
             else:
-                nc.vector.tensor_scalar_mul(out=hs_rows[:, b, :], in0=h_bias[:, b, :], scalar1=dinv[:, b : b + 1])
+                nc.vector.tensor_scalar_mul(out=hs_pairs[:, b // 2, :, b % 2], in0=h_bias[:, b, :], scalar1=dinv[:, b : b + 1])
 
         def group_hs(c):
             nc.vector.tensor_copy(
-                out=hs_grouped[:, c, :, :].rearrange("p (r i) t -> p r t i", i=4),
-                in_=hs_rows[:, 4 * c : 4 * c + 4, :].rearrange("p t (r i) -> p r t i", i=4),
+                out=hs_grouped[:, c, :, :].bitcast(F32),
+                in_=hs_pairs[:, 2 * c : 2 * c + 2, :, :].bitcast(F32).rearrange("p u f w -> p f (u w)"),
             )
 
         def quantise_hs(c):
@@ -230,7 +234,7 @@ def tile_gcnlayer_pa_kernel(tc, x, adj, W1_words, W1_scales, b1, ln_gamma, ln_be
 
         def mean(b):
             one = slice(b, b + 1)
-            nc.gpsimd.tensor_scalar(out=minus_mean[:, one], in0=g_sum[:, one], scalar1=-1.0 / FEAT, scalar2=0.0, op0=ALU.mult, op1=ALU.add)
+            nc.scalar.mul(out=minus_mean[:, one], in_=g_sum[:, one], mul=-1.0 / FEAT)
 
         def sum_of_squares(b):
             one = slice(b, b + 1)
@@ -259,13 +263,6 @@ def tile_gcnlayer_pa_kernel(tc, x, adj, W1_words, W1_scales, b1, ln_gamma, ln_be
                 op0=ALU.add,
                 op1=ALU.mult,
             )
-
-        def finish_gpsimd(b):
-            nc.gpsimd.tensor_scalar(
-                out=scaled[:, b, :], in0=scaled[:, b, :], scalar1=rstd[:, b : b + 1], scalar2=0.0, op0=ALU.mult, op1=ALU.add
-            )
-            nc.gpsimd.tensor_tensor(out=result[:, b, :], in0=scaled[:, b, :], in1=beta_all[:], op=ALU.add)
-            nc.sync.dma_start(out=out_view[:, b // 2, b % 2, :], in_=result[:, b, :])
 
         def finish(b):
             nc.vector.scalar_tensor_tensor(
@@ -316,45 +313,47 @@ def tile_gcnlayer_pa_kernel(tc, x, adj, W1_words, W1_scales, b1, ln_gamma, ln_be
         turn_x(1)
         b1_ps = acc.tile([P, BANK], F32, tag="acc")
         spread(0, b1_ps[:, 0:FEAT])
+        nc.scalar.copy(out=b1_all[:], in_=b1_ps[:, 0:FEAT])
         turn_x(2)
-        turn_x(3)
         quantise_x(0)
-        nc.vector.tensor_copy(out=b1_all[:], in_=b1_ps[:, 0:FEAT])
         quantise_x(1)
         first_product(0)
         first_product(1)
+        turn_x(3)
         quantise_x(2)
         first_product(2)
-        quantise_x(3)
         first_product(3)
+        quantise_x(3)
         row_sum_scalar(0)
-        turn_adj(2)
-        turn_adj(3)
         first_product(4)
         first_product(5)
+        turn_adj(2)
+        turn_adj(3)
         row_sum_scalar(1)
         first_product(6)
         first_product(7)
         row_sum(2)
         row_sum(3)
-        tensor_degrees()
         row_sum_vector(4)
+        tensor_degrees2()
         row_sum_scalar(5)
         row_sum_vector(6)
         row_sum_vector(7)
-        degrees(1)
+        degrees(4, 4)
+
+        turn_adj(0)
         quantise_adj(2)
         scale_hs(2)
         scale_hs(3)
+        quantise_adj(3)
         scale_hs(0)
         scale_hs(1)
-        turn_adj(0)
         scale_hs(4)
         scale_hs(5)
-        quantise_adj(3)
+        quantise_adj(0)
+        group_hs(0)
         turn_adj(1)
         turn_adj(4)
-        group_hs(0)
         scale_hs(6)
         scale_hs(7)
         turn_adj(5, acc, "acc")
@@ -364,8 +363,8 @@ def tile_gcnlayer_pa_kernel(tc, x, adj, W1_words, W1_scales, b1, ln_gamma, ln_be
         group_hs(1)
         spread(1, gamma_beta[:, 0, :])
         spread(2, gamma_beta[:, 1, :])
-        quantise_adj(0)
         quantise_hs(1)
+        quantise_adj(1)
 
         products = {0: second_product(ORDER[0])}
         for s in range(BLOCKS + FINISH_LAG):
@@ -374,18 +373,15 @@ def tile_gcnlayer_pa_kernel(tc, x, adj, W1_words, W1_scales, b1, ln_gamma, ln_be
             if s < BLOCKS:
                 add_hs(ORDER[s], products[s])
                 gelu_and_mean(ORDER[s])
-                mean(ORDER[s])
             if 1 <= s <= BLOCKS:
                 sum_of_squares(ORDER[s - 1])
-
-            if s + 3 < BLOCKS:
-                quantise_adj(ORDER[s + 3])
+            if s < BLOCKS:
+                mean(ORDER[s])
+            if s + 4 < BLOCKS:
+                quantise_adj(ORDER[s + 4])
+            if FINISH_LAG <= s:
+                finish(ORDER[s - FINISH_LAG])
             if 2 <= s < BLOCKS + 2:
                 centre_and_gain(ORDER[s - 2])
-            if FINISH_LAG <= s:
-                if s - FINISH_LAG in ():
-                    finish_gpsimd(ORDER[s - FINISH_LAG])
-                else:
-                    finish(ORDER[s - FINISH_LAG])
             if s in (2, 4, 6, 8):
                 inverse_std(ORDER[s - 2], 2)

@@ -16,8 +16,6 @@ NODES = 1024
 K_IN = 512
 FEAT = 384
 EPS = 1e-6
-SELF_LOOP = 16
-ROW = NODES + SELF_LOOP
 BLOCKS = NODES // P
 PASSES = NODES // (P * PACK)
 CHUNKS = BLOCKS // 2
@@ -25,7 +23,7 @@ BANK = 512
 FEAT_CUTS = ((0, 256), (256, 128))
 FINISH_LAG = 6
 TENSOR_CHUNKS = (1, 2)
-ORDER = (2, 3, 0, 1, 4, 5, 6, 7)
+ORDER = (0, 1, 2, 3, 4, 5, 6, 7)
 
 FLOPS = 2 * NODES * K_IN * FEAT + 2 * NODES * NODES * FEAT
 
@@ -41,7 +39,7 @@ def tile_gcnlayer_pa_kernel(tc, x, adj, W1_words, W1_scales, b1, ln_gamma, ln_be
         name="fixed", bufs=1
     ) as fixed, tc.psum_pool(name="turn", bufs=3) as turn, tc.psum_pool(name="acc", bufs=4) as acc:
         x_sb = keep.tile([P, BLOCKS, K_IN], BF16)
-        adj_sb = keep.tile([P, BLOCKS, ROW], BF16)
+        adj_sb = keep.tile([P, BLOCKS, NODES], BF16)
         w_codes = keep.tile([P, FEAT], U32, align_bytes=64)
         w_scales = keep.tile([P, FEAT], U8, align_bytes=64)
 
@@ -65,11 +63,12 @@ def tile_gcnlayer_pa_kernel(tc, x, adj, W1_words, W1_scales, b1, ln_gamma, ln_be
         deg_ps = shared_bank[:, FEAT : FEAT + BLOCKS]
         minus_half = keep.tile([P, BLOCKS], F32)
         table_in = keep.tile([P, 1], F32)
-        table_out = keep.tile([P, 1], F32)
+        table_out = keep.tile([P, 2], F32)
 
-        row_copy = keep.tile([P, BLOCKS, ROW], BF16)
-        pair_sums = keep.tile([P, 2, ROW // 2], F32)
+        row_copy = keep.tile([P, BLOCKS, NODES], BF16)
+        pair_sums = keep.tile([P, 2, NODES // 2], F32)
         deg = keep.tile([P, BLOCKS, 8], F32)
+        root = keep.tile([P, BLOCKS], F32)
         dinv = keep.tile([P, BLOCKS], F32)
 
         h_bias = keep.tile([P, BLOCKS, FEAT], F32)
@@ -120,6 +119,9 @@ def tile_gcnlayer_pa_kernel(tc, x, adj, W1_words, W1_scales, b1, ln_gamma, ln_be
                     start=True,
                     stop=True,
                 )
+            return h_ps
+
+        def add_bias(b, h_ps):
             nc.vector.tensor_tensor(out=h_bias[:, b, :], in0=h_ps[:], in1=b1_all[:], op=ALU.add)
 
         def row_sum(b):
@@ -133,18 +135,14 @@ def tile_gcnlayer_pa_kernel(tc, x, adj, W1_words, W1_scales, b1, ln_gamma, ln_be
                         stop=(c == PASSES - 1 and t == PACK - 1),
                     )
 
-        def degrees(b, count):
+        def roots(b, count, from_tensor):
             some = slice(b, b + count)
-            nc.gpsimd.tensor_tensor(out=dinv[:, some], in0=deg[:, some, 0], in1=minus_half[:, 0:count], op=ALU.pow)
+            sums = deg_ps[:, some] if from_tensor else deg[:, some, 0]
+            nc.scalar.activation(out=root[:, some], in_=sums, func=ACT.Sqrt, bias=1.0)
 
-        def tensor_degrees(b, count):
+        def invert(b, count):
             some = slice(b, b + count)
-            nc.scalar.add(out=deg[:, some, 0], in_=deg_ps[:, some], add=1.0)
-            degrees(b, count)
-
-        def tensor_degrees2():
-            nc.scalar.add(out=deg[:, 2:4, 0], in_=deg_ps[:, 2:4], add=1.0)
-            degrees(0, 4)
+            nc.vector.reciprocal(out=dinv[:, some], in_=root[:, some])
 
         def row_sum_scalar(b):
             nc.scalar.activation(out=row_copy[:, b, :], in_=adj_sb[:, b, :], func=ACT.Copy, accum_out=deg[:, b, 0:1])
@@ -153,16 +151,16 @@ def tile_gcnlayer_pa_kernel(tc, x, adj, W1_words, W1_scales, b1, ln_gamma, ln_be
             row = adj_sb[:, b, :]
             nc.vector.scalar_tensor_tensor(
                 out=pair_sums[:, b % 2, :],
-                in0=row[:, 0 : ROW // 2],
+                in0=row[:, 0 : NODES // 2],
                 scalar=1.0,
-                in1=row[:, ROW // 2 : ROW],
+                in1=row[:, NODES // 2 : NODES],
                 op0=ALU.mult,
                 op1=ALU.add,
                 accum_out=deg[:, b, 0:1],
             )
 
-        def turn_adj(b, pool=turn, tag="turn"):
-            adj_words = adj_sb[:, b, 0:NODES].bitcast(F32)
+        def turn_adj(b, pool=turn, tag="turn", copy=nc.scalar.copy):
+            adj_words = adj_sb[:, b, :].bitcast(F32)
             adj_turned = pool.tile([P, PASSES, 2, P], F32, tag=tag)
             for c in range(PASSES):
                 for u in range(2):
@@ -170,7 +168,7 @@ def tile_gcnlayer_pa_kernel(tc, x, adj, W1_words, W1_scales, b1, ln_gamma, ln_be
                     nc.tensor.transpose(
                         out=adj_turned[:, c, u, :], in_=adj_words[:, first : first + P], identity=identity[:]
                     )
-            nc.scalar.copy(
+            copy(
                 out=adj_grouped[:, b, :, :, :].bitcast(F32), in_=adj_turned[:].rearrange("p c u i -> p c i u")
             )
 
@@ -247,11 +245,12 @@ def tile_gcnlayer_pa_kernel(tc, x, adj, W1_words, W1_scales, b1, ln_gamma, ln_be
                 accum_out=square_sum[:, one],
             )
 
+        def variance(b, count):
+            both = slice(b, b + count)
+            nc.scalar.activation(out=var_eps[:, both], in_=square_sum[:, both], func=ACT.Identity, scale=1.0 / FEAT**3, bias=EPS)
+
         def inverse_std(b, count):
             both = slice(b, b + count)
-            nc.gpsimd.tensor_scalar(
-                out=var_eps[:, both], in0=square_sum[:, both], scalar1=1.0 / FEAT**3, scalar2=EPS, op0=ALU.mult, op1=ALU.add
-            )
             nc.gpsimd.tensor_tensor(out=rstd[:, both], in0=var_eps[:, both], in1=minus_half[:, 0:count], op=ALU.pow)
 
         def centre_and_gain(b):
@@ -281,17 +280,17 @@ def tile_gcnlayer_pa_kernel(tc, x, adj, W1_words, W1_scales, b1, ln_gamma, ln_be
             nc.vector.memset(vector_rows[:, v, :].bitcast(U32), 0)
         nc.vector.memset(ones[:], 1.0)
         nc.vector.memset(minus_half[:], -0.5)
-        nc.vector.memset(adj_sb[:, :, NODES:ROW], 0.0)
-        nc.vector.memset(adj_sb[:, :, NODES : NODES + 1], 1.0)
         make_identity(nc, identity[:])
-        nc.scalar.activation(out=table_out[:], in_=table_in[:], func=ACT.Gelu)
+        nc.scalar.activation(out=table_out[:, 0:1], in_=table_in[:], func=ACT.Sqrt)
 
         def load_x(q):
             nc.sync.dma_start(out=x_sb[:, 2 * q : 2 * q + 2, :], in_=x_view[:, q, :, :])
 
         def load_adj(q):
-            nc.sync.dma_start(out=adj_sb[:, 2 * q : 2 * q + 2, 0:NODES], in_=adj_view[:, q, :, :])
+            nc.sync.dma_start(out=adj_sb[:, 2 * q : 2 * q + 2, :], in_=adj_view[:, q, :, :])
 
+        for v, vector in enumerate((b1, ln_gamma, ln_beta)):
+            nc.gpsimd.dma_start(out=vector_rows[0:1, v, :], in_=vector.unsqueeze(0))
         load_x(0)
         load_x(1)
         nc.sync.dma_start(
@@ -302,12 +301,12 @@ def tile_gcnlayer_pa_kernel(tc, x, adj, W1_words, W1_scales, b1, ln_gamma, ln_be
                 out=w_scales[32 * quadrant : 32 * quadrant + 4, :].bitcast(I32),
                 in_=W1_scales[0, 4 * quadrant : 4 * quadrant + 4, :].bitcast(I32),
             )
-        for v, vector in enumerate((b1, ln_gamma, ln_beta)):
-            nc.gpsimd.dma_start(out=vector_rows[0:1, v, :], in_=vector.unsqueeze(0))
         load_x(2)
         load_x(3)
-        for q in range(CHUNKS):
-            load_adj(q)
+        load_adj(0)
+        load_adj(1)
+        load_adj(2)
+        load_adj(3)
 
         turn_x(0)
         turn_x(1)
@@ -317,54 +316,60 @@ def tile_gcnlayer_pa_kernel(tc, x, adj, W1_words, W1_scales, b1, ln_gamma, ln_be
         turn_x(2)
         quantise_x(0)
         quantise_x(1)
-        first_product(0)
-        first_product(1)
+        h = [first_product(0), first_product(1)]
         turn_x(3)
+        add_bias(0, h[0])
+        add_bias(1, h[1])
         quantise_x(2)
-        first_product(2)
-        first_product(3)
+        h += [first_product(2), first_product(3)]
+        turn_adj(0)
+        add_bias(2, h[2])
+        add_bias(3, h[3])
         quantise_x(3)
-        row_sum_scalar(0)
-        first_product(4)
-        first_product(5)
+        h += [first_product(4), first_product(5)]
+        turn_adj(1)
         turn_adj(2)
+        add_bias(4, h[4])
+        add_bias(5, h[5])
+        h += [first_product(6), first_product(7)]
         turn_adj(3)
-        row_sum_scalar(1)
-        first_product(6)
-        first_product(7)
+        add_bias(6, h[6])
+        add_bias(7, h[7])
+        row_sum(0)
+        row_sum(1)
         row_sum(2)
         row_sum(3)
-        row_sum_vector(4)
-        tensor_degrees2()
-        row_sum_scalar(5)
+        row_sum_scalar(4)
+        roots(0, 4, True)
+        row_sum_vector(5)
         row_sum_vector(6)
         row_sum_vector(7)
-        degrees(4, 4)
-
-        turn_adj(0)
-        quantise_adj(2)
+        turn_adj(4)
+        invert(0, 4)
         scale_hs(2)
         scale_hs(3)
-        quantise_adj(3)
+        roots(4, 4, False)
         scale_hs(0)
         scale_hs(1)
-        scale_hs(4)
-        scale_hs(5)
+        invert(4, 4)
         quantise_adj(0)
-        group_hs(0)
-        turn_adj(1)
-        turn_adj(4)
         scale_hs(6)
         scale_hs(7)
-        turn_adj(5, acc, "acc")
-        turn_adj(6, acc, "acc")
-        turn_adj(7, acc, "acc")
+        group_hs(0)
+        scale_hs(4)
+        scale_hs(5)
+        quantise_adj(1)
         quantise_hs(0)
         group_hs(1)
+        nc.scalar.activation(out=table_out[:, 1:2], in_=table_in[:], func=ACT.Gelu)
+        turn_adj(5)
+        turn_adj(6)
+        quantise_adj(2)
+        quantise_hs(1)
         spread(1, gamma_beta[:, 0, :])
         spread(2, gamma_beta[:, 1, :])
-        quantise_hs(1)
-        quantise_adj(1)
+        turn_adj(7, acc, "acc", nc.vector.tensor_copy)
+        quantise_adj(3)
 
         products = {0: second_product(ORDER[0])}
         for s in range(BLOCKS + FINISH_LAG):
@@ -373,15 +378,19 @@ def tile_gcnlayer_pa_kernel(tc, x, adj, W1_words, W1_scales, b1, ln_gamma, ln_be
             if s < BLOCKS:
                 add_hs(ORDER[s], products[s])
                 gelu_and_mean(ORDER[s])
+            if s in (3, 5, 7):
+                variance(ORDER[s - 3], 2)
+                inverse_std(ORDER[s - 3], 2)
             if 1 <= s <= BLOCKS:
                 sum_of_squares(ORDER[s - 1])
             if s < BLOCKS:
                 mean(ORDER[s])
+            if s == BLOCKS:
+                variance(ORDER[6], 2)
+                inverse_std(ORDER[6], 2)
             if s + 4 < BLOCKS:
                 quantise_adj(ORDER[s + 4])
             if FINISH_LAG <= s:
                 finish(ORDER[s - FINISH_LAG])
             if 2 <= s < BLOCKS + 2:
                 centre_and_gain(ORDER[s - 2])
-            if s in (2, 4, 6, 8):
-                inverse_std(ORDER[s - 2], 2)

@@ -56,6 +56,7 @@ def tile_gcnlayer_pa_kernel(tc, x, adj, W1_words, W1_scales, b1, ln_gamma, ln_be
 
         identity = keep.tile([P, P], F32)
         ones = keep.tile([P, P], BF16)
+        idle_rows = keep.tile([P, FEAT], BF16)
         vector_rows = keep.tile([P, 3, FEAT], BF16)
         b1_all = keep.tile([P, FEAT], F32)
         shared_bank = fixed.tile([P, BANK], F32)
@@ -275,10 +276,11 @@ def tile_gcnlayer_pa_kernel(tc, x, adj, W1_words, W1_scales, b1, ln_gamma, ln_be
             nc.sync.dma_start(out=out_view[:, b // 2, b % 2, :], in_=result[:, b, :])
 
         nc.vector.memset(table_in[:], 0.0)
+        nc.vector.memset(ones[:], 1.0)
+        nc.vector.memset(idle_rows[:], 0.0)
         nc.vector.memset(w_scales[:].bitcast(I32), 0)
         for v in range(3):
             nc.vector.memset(vector_rows[:, v, :].bitcast(U32), 0)
-        nc.vector.memset(ones[:], 1.0)
         nc.vector.memset(minus_half[:], -0.5)
         make_identity(nc, identity[:])
         nc.scalar.activation(out=table_out[:, 0:1], in_=table_in[:], func=ACT.Sqrt)
@@ -308,6 +310,9 @@ def tile_gcnlayer_pa_kernel(tc, x, adj, W1_words, W1_scales, b1, ln_gamma, ln_be
         load_adj(2)
         load_adj(3)
 
+        idle_ps = acc.tile([P, BANK], F32, tag="acc")
+        for i in range(6):
+            nc.tensor.matmul(out=idle_ps[:, 0:FEAT], lhsT=ones[:], rhs=idle_rows[:], start=True, stop=True)
         turn_x(0)
         turn_x(1)
         b1_ps = acc.tile([P, BANK], F32, tag="acc")
@@ -326,13 +331,14 @@ def tile_gcnlayer_pa_kernel(tc, x, adj, W1_words, W1_scales, b1, ln_gamma, ln_be
         add_bias(2, h[2])
         add_bias(3, h[3])
         quantise_x(3)
-        h += [first_product(4), first_product(5)]
         turn_adj(1)
+        h += [first_product(4), first_product(5)]
         turn_adj(2)
+        turn_adj(3)
         add_bias(4, h[4])
         add_bias(5, h[5])
         h += [first_product(6), first_product(7)]
-        turn_adj(3)
+        row_sum_vector(5)
         add_bias(6, h[6])
         add_bias(7, h[7])
         row_sum(0)
@@ -341,7 +347,6 @@ def tile_gcnlayer_pa_kernel(tc, x, adj, W1_words, W1_scales, b1, ln_gamma, ln_be
         row_sum(3)
         row_sum_scalar(4)
         roots(0, 4, True)
-        row_sum_vector(5)
         row_sum_vector(6)
         row_sum_vector(7)
         turn_adj(4)

import concourse.mybir as mybir
from concourse.masks import make_identity

F32 = mybir.dt.float32
BF16 = mybir.dt.bfloat16
I32 = mybir.dt.int32
U32 = mybir.dt.uint32
U8 = mybir.dt.uint8
FP8X4 = mybir.dt.float8_e4m3fn_x4
ALU = mybir.AluOpType
ACT = mybir.ActivationFunctionType

P = 128
PACK = 4
NODES = 1024
K_IN = 512
FEAT = 384
EPS = 1e-6
BLOCKS = NODES // P
PASSES = NODES // (P * PACK)
CHUNKS = BLOCKS // 2
BANK = 512
FEAT_CUTS = ((0, 256), (256, 128))
FINISH_LAG = 6
TENSOR_CHUNKS = (1, 2)
ORDER = (0, 1, 2, 3, 4, 5, 6, 7)

FLOPS = 2 * NODES * K_IN * FEAT + 2 * NODES * NODES * FEAT


def tile_gcnlayer_pa_kernel(tc, x, adj, W1_words, W1_scales, b1, ln_gamma, ln_beta, out):
    nc = tc.nc

    x_view = x.rearrange("(q p e) k -> p q e k", q=CHUNKS, p=P, e=2)
    adj_view = adj.rearrange("(q p e) j -> p q e j", q=CHUNKS, p=P, e=2)
    out_view = out.rearrange("(q p e) f -> p q e f", q=CHUNKS, p=P, e=2)

    with tc.manual_schedule(), tc.tile_pool(name="keep", bufs=1) as keep, tc.psum_pool(
        name="fixed", bufs=1
    ) as fixed, tc.psum_pool(name="turn", bufs=3) as turn, tc.psum_pool(name="acc", bufs=4) as acc:
        x_sb = keep.tile([P, BLOCKS, K_IN], BF16)
        adj_sb = keep.tile([P, BLOCKS, NODES], BF16)
        w_codes = keep.tile([P, FEAT], U32, align_bytes=64)
        w_scales = keep.tile([P, FEAT], U8, align_bytes=64)

        x_grouped = keep.tile([P, BLOCKS, P, PACK], BF16, align_bytes=64)
        x_codes = keep.tile([P, BLOCKS, P], U32, align_bytes=64)
        x_scales = keep.tile([P, BLOCKS, P], U8, align_bytes=64)
        adj_grouped = keep.tile([P, BLOCKS, PASSES, P, PACK], BF16, align_bytes=64)
        adj_codes = keep.tile([P, BLOCKS, PASSES, P], U32, align_bytes=64)
        adj_scales = keep.tile([P, BLOCKS, PASSES, P], U8, align_bytes=64)
        hs_pairs = keep.tile([P, CHUNKS, FEAT, 2], BF16)
        hs_grouped = keep.tile([P, PASSES, FEAT, PACK], BF16, align_bytes=64)
        hs_codes = keep.tile([P, PASSES, FEAT], U32, align_bytes=64)
        hs_scales = keep.tile([P, PASSES, FEAT], U8, align_bytes=64)

        identity = keep.tile([P, P], F32)
        ones = keep.tile([P, P], BF16)
        idle_rows = keep.tile([P, FEAT], BF16)
        vector_rows = keep.tile([P, 3, FEAT], BF16)
        b1_all = keep.tile([P, FEAT], F32)
        shared_bank = fixed.tile([P, BANK], F32)
        gamma_beta = shared_bank[:, 0:FEAT].bitcast(BF16).rearrange("p (v f) -> p v f", v=2)
        deg_ps = shared_bank[:, FEAT : FEAT + BLOCKS]
        minus_half = keep.tile([P, BLOCKS], F32)
        table_in = keep.tile([P, 1], F32)
        table_out = keep.tile([P, 2], F32)

        row_copy = keep.tile([P, BLOCKS, NODES], BF16)
        pair_sums = keep.tile([P, 2, NODES // 2], F32)
        deg = keep.tile([P, BLOCKS, 8], F32)
        root = keep.tile([P, BLOCKS], F32)
        dinv = keep.tile([P, BLOCKS], F32)

        h_bias = keep.tile([P, BLOCKS, FEAT], F32)
        pre = keep.tile([P, BLOCKS, FEAT], F32)
        g = keep.tile([P, BLOCKS, FEAT], F32)
        squares = keep.tile([P, BLOCKS, FEAT], F32)
        scaled = keep.tile([P, BLOCKS, FEAT], F32)
        result = keep.tile([P, BLOCKS, FEAT], F32)
        g_sum = keep.tile([P, BLOCKS], F32)
        minus_mean = keep.tile([P, BLOCKS], F32)
        square_sum = keep.tile([P, BLOCKS], F32)
        var_eps = keep.tile([P, BLOCKS], F32)
        rstd = keep.tile([P, BLOCKS], F32)

        def spread(v, everywhere):
            nc.tensor.matmul(out=everywhere, lhsT=ones[:], rhs=vector_rows[:, v, :], start=True, stop=True)

        def turn_x(q):
            x_turned = turn.tile([P, 2, 2, P], F32, tag="turn")
            for e in range(2):
                x_words = x_sb[:, 2 * q + e, :].bitcast(F32)
                for u in range(2):
                    nc.tensor.transpose(
                        out=x_turned[:, e, u, :], in_=x_words[:, u : K_IN // 2 : 2], identity=identity[:]
                    )
            nc.scalar.copy(
                out=x_grouped[:, 2 * q : 2 * q + 2, :, :].bitcast(F32),
                in_=x_turned[:].rearrange("p e u n -> p e n u"),
            )

        def quantise_x(q):
            both = slice(2 * q, 2 * q + 2)
            nc.vector.quantize_mx(
                out=x_codes[:, both, :].rearrange("p e n -> p (e n)").bitcast(FP8X4),
                scales=x_scales[:, both, :].rearrange("p e n -> p (e n)"),
                in_=x_grouped[:, both, :, :].rearrange("p e n t -> p (e n t)"),
            )

        def first_product(b):
            h_ps = acc.tile([P, FEAT], F32, tag="acc")
            for f0, width in FEAT_CUTS:
                nc.tensor.matmul_mx(
                    out=h_ps[:, f0 : f0 + width],
                    lhsT=x_codes[:, b, :].bitcast(FP8X4),
                    lhsT_scale=x_scales[:, b, :],
                    rhs=w_codes[:, f0 : f0 + width].bitcast(FP8X4),
                    rhs_scale=w_scales[:, f0 : f0 + width],
                    start=True,
                    stop=True,
                )
            return h_ps

        def add_bias(b, h_ps):
            nc.vector.tensor_tensor(out=h_bias[:, b, :], in0=h_ps[:], in1=b1_all[:], op=ALU.add)

        def row_sum(b):
            for c in range(PASSES):
                for t in range(PACK):
                    nc.tensor.matmul(
                        out=deg_ps[:, b : b + 1],
                        lhsT=adj_grouped[:, b, c, :, t],
                        rhs=ones[:, 0:1],
                        start=(c == 0 and t == 0),
                        stop=(c == PASSES - 1 and t == PACK - 1),
                    )

        def roots(b, count, from_tensor):
            some = slice(b, b + count)
            sums = deg_ps[:, some] if from_tensor else deg[:, some, 0]
            nc.scalar.activation(out=root[:, some], in_=sums, func=ACT.Sqrt, bias=1.0)

        def invert(b, count):
            some = slice(b, b + count)
            nc.vector.reciprocal(out=dinv[:, some], in_=root[:, some])

        def row_sum_scalar(b):
            nc.scalar.activation(out=row_copy[:, b, :], in_=adj_sb[:, b, :], func=ACT.Copy, accum_out=deg[:, b, 0:1])

        def row_sum_vector(b):
            row = adj_sb[:, b, :]
            nc.vector.scalar_tensor_tensor(
                out=pair_sums[:, b % 2, :],
                in0=row[:, 0 : NODES // 2],
                scalar=1.0,
                in1=row[:, NODES // 2 : NODES],
                op0=ALU.mult,
                op1=ALU.add,
                accum_out=deg[:, b, 0:1],
            )

        def turn_adj(b, pool=turn, tag="turn", copy=nc.scalar.copy):
            adj_words = adj_sb[:, b, :].bitcast(F32)
            adj_turned = pool.tile([P, PASSES, 2, P], F32, tag=tag)
            for c in range(PASSES):
                for u in range(2):
                    first = (2 * c + u) * P
                    nc.tensor.transpose(
                        out=adj_turned[:, c, u, :], in_=adj_words[:, first : first + P], identity=identity[:]
                    )
            copy(
                out=adj_grouped[:, b, :, :, :].bitcast(F32), in_=adj_turned[:].rearrange("p c u i -> p c i u")
            )

        def quantise_adj(b):
            nc.vector.quantize_mx(
                out=adj_codes[:, b, :, :].rearrange("p c i -> p (c i)").bitcast(FP8X4),
                scales=adj_scales[:, b, :, :].rearrange("p c i -> p (c i)"),
                in_=adj_grouped[:, b, :, :, :].rearrange("p c i t -> p (c i t)"),
            )

        def scale_hs(b):
            if b in (0, 1, 4, 5):
                nc.scalar.activation(out=hs_pairs[:, b // 2, :, b % 2], in_=h_bias[:, b, :], func=ACT.Copy, scale=dinv[:, b : b + 1])
            else:
                nc.vector.tensor_scalar_mul(out=hs_pairs[:, b // 2, :, b % 2], in0=h_bias[:, b, :], scalar1=dinv[:, b : b + 1])

        def group_hs(c):
            nc.vector.tensor_copy(
                out=hs_grouped[:, c, :, :].bitcast(F32),
                in_=hs_pairs[:, 2 * c : 2 * c + 2, :, :].bitcast(F32).rearrange("p u f w -> p f (u w)"),
            )

        def quantise_hs(c):
            for f0, width in FEAT_CUTS:
                nc.vector.quantize_mx(
                    out=hs_codes[:, c, f0 : f0 + width].bitcast(FP8X4),
                    scales=hs_scales[:, c, f0 : f0 + width],
                    in_=hs_grouped[:, c, f0 : f0 + width, :].rearrange("p f t -> p (f t)"),
                )

        def second_product(b):
            agg_ps = acc.tile([P, FEAT], F32, tag="acc")
            for f0, width in FEAT_CUTS:
                for c in range(PASSES):
                    nc.tensor.matmul_mx(
                        out=agg_ps[:, f0 : f0 + width],
                        lhsT=adj_codes[:, b, c, :].bitcast(FP8X4),
                        lhsT_scale=adj_scales[:, b, c, :],
                        rhs=hs_codes[:, c, f0 : f0 + width].bitcast(FP8X4),
                        rhs_scale=hs_scales[:, c, f0 : f0 + width],
                        start=(c == 0),
                        stop=(c == PASSES - 1),
                    )
            return agg_ps

        def add_hs(b, agg_ps):
            nc.vector.scalar_tensor_tensor(
                out=pre[:, b, :],
                in0=h_bias[:, b, :],
                scalar=dinv[:, b : b + 1],
                in1=agg_ps[:],
                op0=ALU.mult,
                op1=ALU.add,
            )

        def gelu_and_mean(b):
            one = slice(b, b + 1)
            nc.scalar.activation(
                out=g[:, b, :], in_=pre[:, b, :], func=ACT.Gelu, scale=dinv[:, one], accum_out=g_sum[:, one]
            )

        def mean(b):
            one = slice(b, b + 1)
            nc.scalar.mul(out=minus_mean[:, one], in_=g_sum[:, one], mul=-1.0 / FEAT)

        def sum_of_squares(b):
            one = slice(b, b + 1)
            nc.scalar.activation(
                out=squares[:, b, :],
                in_=g[:, b, :],
                func=ACT.Square,
                scale=-1.0 * FEAT,
                bias=g_sum[:, one],
                accum_out=square_sum[:, one],
            )

        def variance(b, count):
            both = slice(b, b + count)
            nc.scalar.activation(out=var_eps[:, both], in_=square_sum[:, both], func=ACT.Identity, scale=1.0 / FEAT**3, bias=EPS)

        def inverse_std(b, count):
            both = slice(b, b + count)
            nc.gpsimd.tensor_tensor(out=rstd[:, both], in0=var_eps[:, both], in1=minus_half[:, 0:count], op=ALU.pow)

        def centre_and_gain(b):
            nc.vector.scalar_tensor_tensor(
                out=scaled[:, b, :],
                in0=g[:, b, :],
                scalar=minus_mean[:, b : b + 1],
                in1=gamma_beta[:, 0, :],
                op0=ALU.add,
                op1=ALU.mult,
            )

        def finish(b):
            nc.vector.scalar_tensor_tensor(
                out=result[:, b, :],
                in0=scaled[:, b, :],
                scalar=rstd[:, b : b + 1],
                in1=gamma_beta[:, 1, :],
                op0=ALU.mult,
                op1=ALU.add,
            )
            nc.sync.dma_start(out=out_view[:, b // 2, b % 2, :], in_=result[:, b, :])

        nc.vector.memset(table_in[:], 0.0)
        nc.vector.memset(ones[:], 1.0)
        nc.vector.memset(idle_rows[:], 0.0)
        nc.vector.memset(w_scales[:].bitcast(I32), 0)
        for v in range(3):
            nc.vector.memset(vector_rows[:, v, :].bitcast(U32), 0)
        nc.vector.memset(minus_half[:], -0.5)
        make_identity(nc, identity[:])
        nc.scalar.activation(out=table_out[:, 0:1], in_=table_in[:], func=ACT.Sqrt)

        def load_x(q):
            nc.sync.dma_start(out=x_sb[:, 2 * q : 2 * q + 2, :], in_=x_view[:, q, :, :])

        def load_adj(q):
            nc.sync.dma_start(out=adj_sb[:, 2 * q : 2 * q + 2, :], in_=adj_view[:, q, :, :])

        for v, vector in enumerate((b1, ln_gamma, ln_beta)):
            nc.gpsimd.dma_start(out=vector_rows[0:1, v, :], in_=vector.unsqueeze(0))
        load_x(0)
        load_x(1)
        nc.sync.dma_start(
            out=w_codes[:].bitcast(I32), in_=W1_words.rearrange("g p n t -> (g p) (n t)").bitcast(I32)
        )
        for quadrant in range(4):
            nc.sync.dma_start(
                out=w_scales[32 * quadrant : 32 * quadrant + 4, :].bitcast(I32),
                in_=W1_scales[0, 4 * quadrant : 4 * quadrant + 4, :].bitcast(I32),
            )
        load_x(2)
        load_x(3)
        load_adj(0)
        load_adj(1)
        load_adj(2)
        load_adj(3)

        idle_ps = acc.tile([P, BANK], F32, tag="acc")
        for i in range(6):
            nc.tensor.matmul(out=idle_ps[:, 0:FEAT], lhsT=ones[:], rhs=idle_rows[:], start=True, stop=True)
        turn_x(0)
        turn_x(1)
        b1_ps = acc.tile([P, BANK], F32, tag="acc")
        spread(0, b1_ps[:, 0:FEAT])
        nc.scalar.copy(out=b1_all[:], in_=b1_ps[:, 0:FEAT])
        turn_x(2)
        quantise_x(0)
        quantise_x(1)
        h = [first_product(0), first_product(1)]
        turn_x(3)
        add_bias(0, h[0])
        add_bias(1, h[1])
        quantise_x(2)
        h += [first_product(2), first_product(3)]
        turn_adj(0)
        add_bias(2, h[2])
        add_bias(3, h[3])
        quantise_x(3)
        turn_adj(1)
        h += [first_product(4), first_product(5)]
        turn_adj(2)
        turn_adj(3)
        add_bias(4, h[4])
        add_bias(5, h[5])
        h += [first_product(6), first_product(7)]
        row_sum_vector(5)
        add_bias(6, h[6])
        add_bias(7, h[7])
        row_sum(0)
        row_sum(1)
        row_sum(2)
        row_sum(3)
        row_sum_scalar(4)
        roots(0, 4, True)
        row_sum_vector(6)
        row_sum_vector(7)
        turn_adj(4)
        invert(0, 4)
        scale_hs(2)
        scale_hs(3)
        roots(4, 4, False)
        scale_hs(0)
        scale_hs(1)
        invert(4, 4)
        quantise_adj(0)
        scale_hs(6)
        scale_hs(7)
        group_hs(0)
        scale_hs(4)
        scale_hs(5)
        quantise_adj(1)
        quantise_hs(0)
        group_hs(1)
        nc.scalar.activation(out=table_out[:, 1:2], in_=table_in[:], func=ACT.Gelu)
        turn_adj(5)
        turn_adj(6)
        quantise_adj(2)
        quantise_hs(1)
        spread(1, gamma_beta[:, 0, :])
        spread(2, gamma_beta[:, 1, :])
        turn_adj(7, acc, "acc", nc.vector.tensor_copy)
        quantise_adj(3)

        products = {0: second_product(ORDER[0])}
        for s in range(BLOCKS + FINISH_LAG):
            if s + 1 < BLOCKS:
                products[s + 1] = second_product(ORDER[s + 1])
            if s < BLOCKS:
                add_hs(ORDER[s], products[s])
                gelu_and_mean(ORDER[s])
            if s in (3, 5, 7):
                variance(ORDER[s - 3], 2)
                inverse_std(ORDER[s - 3], 2)
            if 1 <= s <= BLOCKS:
                sum_of_squares(ORDER[s - 1])
            if s < BLOCKS:
                mean(ORDER[s])
            if s == BLOCKS:
                variance(ORDER[6], 2)
                inverse_std(ORDER[6], 2)
            if s + 4 < BLOCKS:
                quantise_adj(ORDER[s + 4])
            if FINISH_LAG <= s:
                finish(ORDER[s - FINISH_LAG])
            if 2 <= s < BLOCKS + 2:
                centre_and_gain(ORDER[s - 2])
